import numpy as np
import ml_dtypes


def mxq(x, axis, fmt="e4m3"):
    dtype, down = {"e4m3": (ml_dtypes.float8_e4m3fn, 7), "e5m2": (ml_dtypes.float8_e5m2, 14)}[fmt]
    v = np.moveaxis(np.asarray(x, np.float32).astype(ml_dtypes.bfloat16).astype(np.float64), axis, -1)
    blocks = v.reshape(v.shape[:-1] + (-1, 32))
    amax = np.abs(blocks).max(-1, keepdims=True)
    byte = np.maximum(np.where(amax > 0, np.frexp(amax)[1] - 1 + 127, 0) - down, 1)
    scale = np.exp2(byte - 127.0)
    codes = (blocks / scale).astype(np.float32).astype(dtype).astype(np.float64)
    return np.moveaxis((codes * scale).reshape(v.shape), -1, axis)


WIDE = False


def mx_kscale(k):
    if not WIDE:
        return np.ones(k)
    levels = np.array([10, -10, 5, -5, 0])
    a = np.random.permutation(np.resize(levels, k // 512 * 4)).reshape(k // 512, 4)
    idx = np.arange(k)
    return np.exp2(a[idx // 512, idx % 128 // 32])


BF16 = ml_dtypes.bfloat16


def bf(x):
    return np.asarray(x, np.float32).astype(BF16)


def f64(x):
    return np.asarray(x).astype(np.float64)


B, C, N, G1, G2 = 2, 8, 1024, 128, 1024
LSCALE = 0.001
EPS = 1e-8
RHO = 4.0
MISS = 0.125
Q = 2 ** 7


def whole(a):
    return np.where(a < 2 * Q, a, (Q + (a - 2 * Q) % Q) * np.exp2((a - 2 * Q) // Q + 1))


def grid(g, p):
    i = np.arange(g) - g // 2
    return np.sign(i) * whole(np.abs(i)) * p


def setup_inputs():
    e = 2.0 * np.abs(np.log2(mx_kscale(N)))
    near = e == 0.0
    hx, hy = float(whole(G1 // 2)), float(whole(G2 // 2))
    cell = 2.0 * np.pi * max(int(near.sum()), 1) / (RHO * 4.0 * hx * hy) * LSCALE * LSCALE
    py = np.exp2(np.round(np.log2(np.sqrt(cell))))
    px = np.exp2(np.round(np.log2(cell / py)))
    grid_lon, grid_lat = grid(G1, px), grid(G2, py)
    x_lon = (np.random.random((B, N)) - 0.5) * 2.0 * hx * px
    x_lat = (np.random.random((B, N)) - 0.5) * 2.0 * hy * py
    side = np.where(np.random.random((B, N)) < 0.5, -1.0, 1.0)
    far = np.where(side > 0.0, grid_lat[-1], grid_lat[0]) + side * (np.sqrt(2.0 * np.log(2.0) * e) + 0.5 * np.random.random((B, N))) * LSCALE
    x_lat = np.where(near, x_lat, far)
    wt = np.random.standard_normal((B, C, N)) * np.exp2(e)
    wt[np.random.random((B, C, N)) < MISS] = np.nan
    return {"x_lon": bf(x_lon), "x_lat": bf(x_lat), "wt": bf(wt), "grid_lon": bf(grid_lon), "grid_lat": bf(grid_lat)}


def reference(x_lon, x_lat, wt, grid_lon, grid_lat):
    x_lon, x_lat, wt, grid_lon, grid_lat = f64(x_lon), f64(x_lat), f64(wt), f64(grid_lon), f64(grid_lat)
    inv2l2 = 0.5 / (LSCALE * LSCALE)
    kx = np.exp(-inv2l2 * (x_lon[:, :, None] - grid_lon[None, None, :]) ** 2)
    ky = np.exp(-inv2l2 * (x_lat[:, :, None] - grid_lat[None, None, :]) ** 2)
    finite = np.isfinite(wt)
    mask = finite.astype(np.float64)
    w = np.where(finite, wt, 0.0)
    kxt = kx.transpose(0, 2, 1)[:, None, :, :]
    kyq = mxq(ky, 1, "e4m3")[:, None, :, :]
    data = mxq(w[:, :, None, :] * kxt, 3, "e4m3") @ kyq
    density = mxq(mask[:, :, None, :] * kxt, 3, "e4m3") @ kyq
    data_norm = data / np.maximum(density, EPS)
    return np.concatenate([data_norm, density], axis=1)

@@ -1,0 +1,299 @@
+from contextlib import ExitStack
+
+import concourse.mybir as mybir
+
+F32 = mybir.dt.float32
+BF16 = mybir.dt.bfloat16
+U32 = mybir.dt.uint32
+U8 = mybir.dt.uint8
+I32 = mybir.dt.int32
+FP8X4 = mybir.dt.float8_e4m3fn_x4
+ACT = mybir.ActivationFunctionType
+ALU = mybir.AluOpType
+
+P = 128
+B, C, N, G1, G2 = 2, 8, 1024, 128, 1024
+PACK = 4
+KP = N // (P * PACK)
+HW = 512
+HH = G2 // HW
+GAMMA = 0.5 / (0.001 * 0.001)
+EPS = 1e-8
+TINY = 1e-18
+FLOPS = 2 * B * (2 * C * G1) * N * G2
+
+DC_ON_SCALAR = ((1, 6), (1, 7))
+
+
+def tile_convcnpweather_t_kernel(tc, x_lon, x_lat, wt, grid_lon, grid_lat, out):
+    nc = tc.nc
+    with ExitStack() as ctx:
+        keep = ctx.enter_context(tc.tile_pool(name="keep", bufs=1))
+        work = ctx.enter_context(tc.tile_pool(name="work", bufs=2))
+        psum = ctx.enter_context(tc.psum_pool(name="psum", bufs=4))
+        ctx.enter_context(tc.manual_schedule())
+
+        xs = keep.tile([P, 2, B * KP, PACK], BF16, name="xs")
+        glon = keep.tile([P, G1], BF16, name="glon")
+        glat = keep.tile([P, G2], BF16, name="glat")
+        wraw = keep.tile([P, B * C * KP, PACK // 2], I32, name="wraw")
+        with nc.allow_non_contiguous_dma(reason="four neighbouring stations go to each partition"):
+            nc.sync.dma_start(out=xs[:, 0], in_=x_lon.rearrange("b (k p t) -> p (b k) t", p=P, t=PACK))
+            nc.scalar.dma_start(out=glon[:], in_=grid_lon.partition_broadcast(P))
+            nc.sync.dma_start(out=xs[:, 1], in_=x_lat.rearrange("b (k p t) -> p (b k) t", p=P, t=PACK))
+            nc.scalar.dma_start(out=glat[:], in_=grid_lat.partition_broadcast(P))
+            nc.sync.dma_start(
+                out=wraw[:],
+                in_=wt.bitcast(I32).rearrange("b c (k p u) -> p (b c k) u", p=P, u=PACK // 2),
+            )
+
+        negx = keep.tile([P, 2, B * KP, PACK], F32, name="negx")
+        tiny = keep.tile([P, 1], F32, name="tiny")
+        nc.vector.memset(tiny[:], TINY)
+        warm = keep.tile([P, 1], F32, name="warm")
+        nc.scalar.activation(out=warm[:], in_=tiny[:], func=ACT.Exp)
+        nc.vector.tensor_scalar(out=negx[:], in0=xs[:], scalar1=-1.0, scalar2=None, op0=ALU.mult)
+
+        kx = keep.tile([P, B, KP, G1, PACK], F32, name="kx")
+        kxb = keep.tile([P, B, KP, G1, PACK], BF16, name="kxb")
+        wbits = keep.tile([P, B, C, KP, PACK], I32, name="wbits")
+        expo = keep.tile([P, B, C, KP, PACK], I32, name="expo")
+        ones = keep.tile([P, B, C, KP, PACK], I32, name="ones")
+        wkeep = keep.tile([P, B, C, KP, PACK], I32, name="wkeep")
+        maskb = keep.tile([P, B, C, KP, PACK], BF16, name="maskb")
+        wfin = wkeep[:].bitcast(F32)
+
+        a_codes = keep.tile([P, B * KP, C * G1], U32, name="a_codes", align_bytes=64)
+        a_scales = keep.tile([P, B * KP, C * G1], U8, name="a_scales", align_bytes=64)
+        m_codes = keep.tile([P, B * KP, C * G1], U32, name="m_codes", align_bytes=64)
+        m_scales = keep.tile([P, B * KP, C * G1], U8, name="m_scales", align_bytes=64)
+        y_codes = keep.tile([P, B * KP, G2], U32, name="y_codes", align_bytes=64)
+        y_scales = keep.tile([P, B * KP, G2], U8, name="y_scales", align_bytes=64)
+        dens = keep.tile([P, B * C, G2], F32, name="dens")
+
+        def weights():
+            flat = "p b c k t -> p (b c k t)"
+            halves = wbits[:].rearrange("p b c k (u e) -> p (b c k u) e", e=2)
+            words = wraw[:].rearrange("p j u -> p (j u)")
+            nc.vector.tensor_scalar(
+                out=halves[:, :, 0], in0=words, scalar1=16, scalar2=None, op0=ALU.logical_shift_left
+            )
+            nc.vector.tensor_scalar(out=halves[:, :, 1], in0=words, scalar1=-65536, scalar2=None, op0=ALU.bitwise_and)
+            nc.vector.tensor_scalar(
+                out=expo[:].rearrange(flat), in0=wbits[:].rearrange(flat), scalar1=23, scalar2=255,
+                op0=ALU.logical_shift_right, op1=ALU.bitwise_and,
+            )
+            nc.vector.tensor_scalar(
+                out=maskb[:].rearrange(flat), in0=expo[:].rearrange(flat), scalar1=255.0, scalar2=None, op0=ALU.is_lt
+            )
+            nc.vector.tensor_scalar(
+                out=ones[:].rearrange(flat), in0=expo[:].rearrange(flat), scalar1=255.0, scalar2=-1.0,
+                op0=ALU.is_lt, op1=ALU.mult,
+            )
+            nc.vector.tensor_tensor(
+                out=wkeep[:].rearrange(flat), in0=wbits[:].rearrange(flat), in1=ones[:].rearrange(flat),
+                op=ALU.bitwise_and,
+            )
+
+        def kx_stage(b):
+            sqx = work.tile([P, KP, PACK, G1], F32, name="sqx", tag="sqx")
+            for k in range(KP):
+                for t in range(PACK):
+                    nc.scalar.activation(
+                        out=sqx[:, k, t, :], in_=glon[:], func=ACT.Square,
+                        bias=negx[:, 0, b * KP + k, t : t + 1], scale=1.0,
+                    )
+            nc.scalar.activation(
+                out=kx[:, b], in_=sqx[:].rearrange("p k t g -> p k g t"), func=ACT.Exp, scale=-GAMMA
+            )
+
+        def kxb_stage(b):
+            nc.vector.tensor_copy(
+                out=kxb[:, b].rearrange("p k g t -> p (k g t)"), in_=kx[:, b].rearrange("p k g t -> p (k g t)")
+            )
+
+        ky_tiles = {}
+
+        def ky_stage(r):
+            b, hh, k = r // 4, (r // 2) % 2, r % 2
+            sq = work.tile([P, PACK, HW], F32, name="sq", tag="sq")
+            for t in range(PACK):
+                nc.scalar.activation(
+                    out=sq[:, t, :], in_=glat[:, hh * HW : (hh + 1) * HW], func=ACT.Square,
+                    bias=negx[:, 1, b * KP + k, t : t + 1], scale=1.0,
+                )
+            kyb = work.tile([P, HW, PACK], BF16, name="kyb", tag="kyb", bufs=3, align_bytes=64)
+            nc.scalar.activation(
+                out=kyb[:].rearrange("p (c i) t -> p c t i", i=4),
+                in_=sq[:].rearrange("p t (c i) -> p c t i", i=4),
+                func=ACT.Exp, scale=-GAMMA,
+            )
+            ky_tiles[r] = kyb
+
+        def qy(r):
+            b, hh, k = r // 4, (r // 2) % 2, r % 2
+            cols = slice(hh * HW, (hh + 1) * HW)
+            nc.vector.quantize_mx(
+                out=y_codes[:, b * KP + k, cols].bitcast(FP8X4),
+                scales=y_scales[:, b * KP + k, cols],
+                in_=ky_tiles[r][:].rearrange("p h t -> p (h t)"),
+            )
+
+        lhs_tiles = {}
+
+        def left(kind, b, k):
+            src, wgt = (kx, wfin) if kind == "a" else (kxb, maskb)
+            prod = work.tile([P, C, G1, PACK], BF16, name="prod", tag="prod", align_bytes=64)
+            nc.vector.tensor_tensor(
+                out=prod[:],
+                in0=src[:, b, k].unsqueeze(1).to_broadcast([P, C, G1, PACK]),
+                in1=wgt[:, b, :, k, :].unsqueeze(2).to_broadcast([P, C, G1, PACK]),
+                op=ALU.mult,
+            )
+            lhs_tiles[(kind, b, k)] = prod
+
+        def qleft(kind, b, k):
+            codes, scales = (a_codes, a_scales) if kind == "a" else (m_codes, m_scales)
+            nc.vector.quantize_mx(
+                out=codes[:, b * KP + k, :].bitcast(FP8X4),
+                scales=scales[:, b * KP + k, :],
+                in_=lhs_tiles[(kind, b, k)][:].rearrange("p c g t -> p (c g t)"),
+            )
+
+        banks = {}
+
+        def group(kind, b, c, hh):
+            codes, scales = (a_codes, a_scales) if kind == "a" else (m_codes, m_scales)
+            acc = psum.tile([P, HW], F32, name="acc_" + kind, tag="acc_" + kind)
+            for k in range(KP):
+                nc.tensor.matmul_mx(
+                    out=acc[:],
+                    lhsT=codes[:, b * KP + k, c * G1 : (c + 1) * G1].bitcast(FP8X4),
+                    lhsT_scale=scales[:, b * KP + k, c * G1 : (c + 1) * G1],
+                    rhs=y_codes[:, b * KP + k, hh * HW : (hh + 1) * HW].bitcast(FP8X4),
+                    rhs_scale=y_scales[:, b * KP + k, hh * HW : (hh + 1) * HW],
+                    start=(k == 0),
+                    stop=(k == KP - 1),
+                )
+            banks[(kind, b, c, hh)] = acc
+
+        def dc(b, c, hh):
+            dst = dens[:, b * C + c, hh * HW : (hh + 1) * HW]
+            if (b, c) in DC_ON_SCALAR:
+                nc.scalar.copy(out=dst, in_=banks[("m", b, c, hh)][:])
+            else:
+                nc.vector.tensor_copy(out=dst, in_=banks[("m", b, c, hh)][:])
+
+        def store_density(b, c):
+            nc.sync.dma_start(out=out[b, C + c], in_=dens[:, b * C + c, :])
+
+        rec_tiles = {}
+
+        def recip(b, c):
+            rec = dens[:, b * C + c, :]
+            nc.scalar.activation(out=rec, in_=rec, func=ACT.Abs_reciprocal_sqrt, bias=tiny[:, 0:1], scale=1.0)
+            nc.scalar.activation(out=rec, in_=rec, func=ACT.Square)
+            rec_tiles[(b, c)] = rec
+
+        def normalise(b, c):
+            res = work.tile([P, G2], F32, name="res", tag="res", bufs=6)
+            for hh in range(HH):
+                cols = slice(hh * HW, (hh + 1) * HW)
+                nc.vector.scalar_tensor_tensor(
+                    out=res[:, cols], in0=rec_tiles[(b, c)][:, cols], scalar=1.0 / EPS,
+                    in1=banks[("a", b, c, hh)][:], op0=ALU.min, op1=ALU.mult,
+                )
+            nc.sync.dma_start(out=out[b, c], in_=res[:])
+
+        kx_stage(0)
+        weights()
+        kx_stage(1)
+        kxb_stage(0)
+        left("m", 0, 0)
+        left("m", 0, 1)
+        qleft("m", 0, 0)
+        qleft("m", 0, 1)
+        ky_stage(0)
+        qy(0)
+        left("a", 0, 0)
+        ky_stage(1)
+        qy(1)
+        for c in range(4):
+            group("m", 0, c, 0)
+        left("a", 0, 1)
+        ky_stage(2)
+        qy(2)
+        for c in range(4):
+            dc(0, c, 0)
+            group("m", 0, c + 4, 0)
+        qleft("a", 0, 0)
+        ky_stage(3)
+        qy(3)
+        qleft("a", 0, 1)
+        for c in range(4):
+            dc(0, c + 4, 0)
+            group("m", 0, c, 1)
+        ky_stage(4)
+        qy(4)
+        for c in range(4):
+            dc(0, c, 1)
+            store_density(0, c)
+            group("m", 0, c + 4, 1)
+        for c in range(4, 6):
+            dc(0, c, 1)
+            store_density(0, c)
+        ky_stage(5)
+        qy(5)
+        for c in range(6, 8):
+            dc(0, c, 1)
+            store_density(0, c)
+        for c in range(2):
+            for hh in range(HH):
+                group("a", 0, c, hh)
+        kxb_stage(1)
+        left("m", 1, 0)
+        ky_stage(6)
+        qy(6)
+        left("m", 1, 1)
+        qleft("m", 1, 0)
+        ky_stage(7)
+        qy(7)
+        qleft("m", 1, 1)
+        for c in range(2):
+            for hh in range(HH):
+                group("m", 1, c, hh)
+        left("a", 1, 0)
+        for c in range(C):
+            recip(0, c)
+
+        def density_round(c):
+            for hh in range(HH):
+                dc(1, c, hh)
+                if c + 2 < C:
+                    group("m", 1, c + 2, hh)
+            store_density(1, c)
+
+        def data_round(b, c):
+            normalise(b, c)
+            nb, ncn = (b, c + 2) if c + 2 < C else (b + 1, c + 2 - C)
+            if nb < B:
+                for hh in range(HH):
+                    group("a", nb, ncn, hh)
+
+        for c in range(4):
+            density_round(c)
+        for c in range(4):
+            data_round(0, c)
+        for c in range(4, 6):
+            density_round(c)
+        left("a", 1, 1)
+        qleft("a", 1, 0)
+        qleft("a", 1, 1)
+        for c in range(4, 8):
+            data_round(0, c)
+        for c in range(6, 8):
+            density_round(c)
+        for c in range(C):
+            recip(1, c)
+        for c in range(C):
+            data_round(1, c)

@@ -22,7 +22,9 @@ EPS = 1e-8
 TINY = 1e-18
 FLOPS = 2 * B * (2 * C * G1) * N * G2
 
-DC_ON_SCALAR = ((1, 6), (1, 7))
+DC_ON_SCALAR = ()
+SQUARE_ON_GPSIMD = ((1, 1), (1, 3), (1, 5), (1, 7))
+LEFT_ON_GPSIMD = (("a", 1, 0), ("a", 1, 1))
 
 
 def tile_convcnpweather_t_kernel(tc, x_lon, x_lat, wt, grid_lon, grid_lat, out):
@@ -144,12 +146,21 @@ def tile_convcnpweather_t_kernel(tc, x_lon, x_lat, wt, grid_lon, grid_lat, out):
         def left(kind, b, k):
             src, wgt = (kx, wfin) if kind == "a" else (kxb, maskb)
             prod = work.tile([P, C, G1, PACK], BF16, name="prod", tag="prod", align_bytes=64)
-            nc.vector.tensor_tensor(
-                out=prod[:],
-                in0=src[:, b, k].unsqueeze(1).to_broadcast([P, C, G1, PACK]),
-                in1=wgt[:, b, :, k, :].unsqueeze(2).to_broadcast([P, C, G1, PACK]),
-                op=ALU.mult,
-            )
+            if (kind, b, k) in LEFT_ON_GPSIMD:
+                for c in range(0, C, 2):
+                    nc.gpsimd.tensor_tensor(
+                        out=prod[:, c : c + 2],
+                        in0=src[:, b, k].unsqueeze(1).to_broadcast([P, 2, G1, PACK]),
+                        in1=wgt[:, b, c : c + 2, k, :].unsqueeze(2).to_broadcast([P, 2, G1, PACK]),
+                        op=ALU.mult,
+                    )
+            else:
+                nc.vector.tensor_tensor(
+                    out=prod[:],
+                    in0=src[:, b, k].unsqueeze(1).to_broadcast([P, C, G1, PACK]),
+                    in1=wgt[:, b, :, k, :].unsqueeze(2).to_broadcast([P, C, G1, PACK]),
+                    op=ALU.mult,
+                )
             lhs_tiles[(kind, b, k)] = prod
 
         def qleft(kind, b, k):
@@ -192,7 +203,10 @@ def tile_convcnpweather_t_kernel(tc, x_lon, x_lat, wt, grid_lon, grid_lat, out):
         def recip(b, c):
             rec = dens[:, b * C + c, :]
             nc.scalar.activation(out=rec, in_=rec, func=ACT.Abs_reciprocal_sqrt, bias=tiny[:, 0:1], scale=1.0)
-            nc.scalar.activation(out=rec, in_=rec, func=ACT.Square)
+            if (b, c) in SQUARE_ON_GPSIMD:
+                nc.gpsimd.tensor_tensor(out=rec, in0=rec, in1=rec, op=ALU.mult)
+            else:
+                nc.scalar.activation(out=rec, in_=rec, func=ACT.Square)
             rec_tiles[(b, c)] = rec
 
         def normalise(b, c):
@@ -262,10 +276,6 @@ def tile_convcnpweather_t_kernel(tc, x_lon, x_lat, wt, grid_lon, grid_lat, out):
         for c in range(2):
             for hh in range(HH):
                 group("m", 1, c, hh)
-        left("a", 1, 0)
-        for c in range(C):
-            recip(0, c)
-
         def density_round(c):
             for hh in range(HH):
                 dc(1, c, hh)
@@ -280,19 +290,20 @@ def tile_convcnpweather_t_kernel(tc, x_lon, x_lat, wt, grid_lon, grid_lat, out):
                 for hh in range(HH):
                     group("a", nb, ncn, hh)
 
+        left("a", 1, 0)
+        left("a", 1, 1)
+        for c in range(C):
+            recip(0, c)
         for c in range(4):
             density_round(c)
         for c in range(4):
             data_round(0, c)
-        for c in range(4, 6):
+        for c in range(4, 8):
             density_round(c)
-        left("a", 1, 1)
         qleft("a", 1, 0)
         qleft("a", 1, 1)
         for c in range(4, 8):
             data_round(0, c)
-        for c in range(6, 8):
-            density_round(c)
         for c in range(C):
             recip(1, c)
         for c in range(C):

@@ -17,14 +17,17 @@ PACK = 4
 KP = N // (P * PACK)
 HW = 512
 HH = G2 // HW
+CH = 4
 GAMMA = 0.5 / (0.001 * 0.001)
 EPS = 1e-8
 TINY = 1e-18
+TINY2 = 1e-30
 FLOPS = 2 * B * (2 * C * G1) * N * G2
 
+V_UNITS = ()
+G_UNITS = ((1, 1), (1, 3), (1, 5), (1, 7))
 DC_ON_SCALAR = ()
-SQUARE_ON_GPSIMD = ((1, 1), (1, 3), (1, 5), (1, 7))
-LEFT_ON_GPSIMD = (("a", 1, 0), ("a", 1, 1))
+A_ON_VECTOR = ((0, 0, 0), (0, 0, 1), (1, 1, 1))
 
 
 def tile_convcnpweather_t_kernel(tc, x_lon, x_lat, wt, grid_lon, grid_lat, out):
@@ -51,9 +54,11 @@ def tile_convcnpweather_t_kernel(tc, x_lon, x_lat, wt, grid_lon, grid_lat, out):
 
         negx = keep.tile([P, 2, B * KP, PACK], F32, name="negx")
         tiny = keep.tile([P, 1], F32, name="tiny")
-        nc.vector.memset(tiny[:], TINY)
+        tiny2 = keep.tile([P, 1], F32, name="tiny2")
         warm = keep.tile([P, 1], F32, name="warm")
+        nc.vector.memset(tiny[:], TINY)
         nc.scalar.activation(out=warm[:], in_=tiny[:], func=ACT.Exp)
+        nc.vector.memset(tiny2[:], TINY2)
         nc.vector.tensor_scalar(out=negx[:], in0=xs[:], scalar1=-1.0, scalar2=None, op0=ALU.mult)
 
         kx = keep.tile([P, B, KP, G1, PACK], F32, name="kx")
@@ -71,7 +76,7 @@ def tile_convcnpweather_t_kernel(tc, x_lon, x_lat, wt, grid_lon, grid_lat, out):
         m_scales = keep.tile([P, B * KP, C * G1], U8, name="m_scales", align_bytes=64)
         y_codes = keep.tile([P, B * KP, G2], U32, name="y_codes", align_bytes=64)
         y_scales = keep.tile([P, B * KP, G2], U8, name="y_scales", align_bytes=64)
-        dens = keep.tile([P, B * C, G2], F32, name="dens")
+        recs = keep.tile([P, B * C, G2], F32, name="recs")
 
         def weights():
             flat = "p b c k t -> p (b c k t)"
@@ -98,7 +103,7 @@ def tile_convcnpweather_t_kernel(tc, x_lon, x_lat, wt, grid_lon, grid_lat, out):
             )
 
         def kx_stage(b):
-            sqx = work.tile([P, KP, PACK, G1], F32, name="sqx", tag="sqx")
+            sqx = work.tile([P, KP, PACK, G1], F32, name="sqx", tag="sqx", bufs=1)
             for k in range(KP):
                 for t in range(PACK):
                     nc.scalar.activation(
@@ -118,7 +123,7 @@ def tile_convcnpweather_t_kernel(tc, x_lon, x_lat, wt, grid_lon, grid_lat, out):
 
         def ky_stage(r):
             b, hh, k = r // 4, (r // 2) % 2, r % 2
-            sq = work.tile([P, PACK, HW], F32, name="sq", tag="sq")
+            sq = work.tile([P, PACK, HW], F32, name="sq", tag="sq", bufs=1)
             for t in range(PACK):
                 nc.scalar.activation(
                     out=sq[:, t, :], in_=glat[:, hh * HW : (hh + 1) * HW], func=ACT.Square,
@@ -143,32 +148,36 @@ def tile_convcnpweather_t_kernel(tc, x_lon, x_lat, wt, grid_lon, grid_lat, out):
 
         lhs_tiles = {}
 
-        def left(kind, b, k):
-            src, wgt = (kx, wfin) if kind == "a" else (kxb, maskb)
-            prod = work.tile([P, C, G1, PACK], BF16, name="prod", tag="prod", align_bytes=64)
-            if (kind, b, k) in LEFT_ON_GPSIMD:
-                for c in range(0, C, 2):
-                    nc.gpsimd.tensor_tensor(
-                        out=prod[:, c : c + 2],
-                        in0=src[:, b, k].unsqueeze(1).to_broadcast([P, 2, G1, PACK]),
-                        in1=wgt[:, b, c : c + 2, k, :].unsqueeze(2).to_broadcast([P, 2, G1, PACK]),
+        def left(kind, b, k, h):
+            c0 = h * CH
+            if kind == "a":
+                prod = work.tile([P, CH, G1, PACK], BF16, name="prod_a", tag="prod_a", bufs=6, align_bytes=64)
+                step = CH if (b, k, h) in A_ON_VECTOR else 2
+                for c in range(0, CH, step):
+                    eng = nc.vector if (b, k, h) in A_ON_VECTOR else nc.gpsimd
+                    eng.tensor_tensor(
+                        out=prod[:, c : c + step],
+                        in0=kx[:, b, k].unsqueeze(1).to_broadcast([P, step, G1, PACK]),
+                        in1=wfin[:, b, c0 + c : c0 + c + step, k, :].unsqueeze(2).to_broadcast([P, step, G1, PACK]),
                         op=ALU.mult,
                     )
             else:
+                prod = work.tile([P, CH, G1, PACK], BF16, name="prod_m", tag="prod_m", bufs=3, align_bytes=64)
                 nc.vector.tensor_tensor(
                     out=prod[:],
-                    in0=src[:, b, k].unsqueeze(1).to_broadcast([P, C, G1, PACK]),
-                    in1=wgt[:, b, :, k, :].unsqueeze(2).to_broadcast([P, C, G1, PACK]),
+                    in0=kxb[:, b, k].unsqueeze(1).to_broadcast([P, CH, G1, PACK]),
+                    in1=maskb[:, b, c0 : c0 + CH, k, :].unsqueeze(2).to_broadcast([P, CH, G1, PACK]),
                     op=ALU.mult,
                 )
-            lhs_tiles[(kind, b, k)] = prod
+            lhs_tiles[(kind, b, k, h)] = prod
 
-        def qleft(kind, b, k):
+        def qleft(kind, b, k, h):
             codes, scales = (a_codes, a_scales) if kind == "a" else (m_codes, m_scales)
+            cols = slice(h * CH * G1, (h + 1) * CH * G1)
             nc.vector.quantize_mx(
-                out=codes[:, b * KP + k, :].bitcast(FP8X4),
-                scales=scales[:, b * KP + k, :],
-                in_=lhs_tiles[(kind, b, k)][:].rearrange("p c g t -> p (c g t)"),
+                out=codes[:, b * KP + k, cols].bitcast(FP8X4),
+                scales=scales[:, b * KP + k, cols],
+                in_=lhs_tiles[(kind, b, k, h)][:].rearrange("p c g t -> p (c g t)"),
             )
 
         banks = {}
@@ -188,100 +197,60 @@ def tile_convcnpweather_t_kernel(tc, x_lon, x_lat, wt, grid_lon, grid_lat, out):
                 )
             banks[(kind, b, c, hh)] = acc
 
-        def dc(b, c, hh):
-            dst = dens[:, b * C + c, hh * HW : (hh + 1) * HW]
-            if (b, c) in DC_ON_SCALAR:
-                nc.scalar.copy(out=dst, in_=banks[("m", b, c, hh)][:])
+        def density(b, c, hh):
+            cols = slice(hh * HW, (hh + 1) * HW)
+            bank = banks[("m", b, c, hh)]
+            if (b, c) in V_UNITS:
+                half = work.tile([P, HW], F32, name="half", tag="half", bufs=4)
+                nc.vector.tensor_copy(out=half[:], in_=bank[:])
+                nc.vector.scalar_tensor_tensor(
+                    out=recs[:, b * C + c, cols], in0=half[:], scalar=1.0, in1=bank[:], op0=ALU.mult, op1=ALU.mult
+                )
+                nc.sync.dma_start(out=out[b, C + c, :, cols], in_=half[:])
             else:
-                nc.vector.tensor_copy(out=dst, in_=banks[("m", b, c, hh)][:])
-
-        def store_density(b, c):
-            nc.sync.dma_start(out=out[b, C + c], in_=dens[:, b * C + c, :])
-
-        rec_tiles = {}
+                if (b, c) in DC_ON_SCALAR:
+                    half = work.tile([P, HW], F32, name="half", tag="half", bufs=4)
+                    nc.scalar.copy(out=half[:], in_=bank[:])
+                    nc.scalar.activation(
+                        out=recs[:, b * C + c, cols], in_=bank[:], func=ACT.Abs_reciprocal_sqrt,
+                        bias=tiny[:, 0:1], scale=1.0,
+                    )
+                    nc.sync.dma_start(out=out[b, C + c, :, cols], in_=half[:])
+                else:
+                    nc.vector.tensor_copy(out=recs[:, b * C + c, cols], in_=bank[:])
+                    if hh == HH - 1:
+                        nc.sync.dma_start(out=out[b, C + c], in_=recs[:, b * C + c, :])
 
         def recip(b, c):
-            rec = dens[:, b * C + c, :]
-            nc.scalar.activation(out=rec, in_=rec, func=ACT.Abs_reciprocal_sqrt, bias=tiny[:, 0:1], scale=1.0)
-            if (b, c) in SQUARE_ON_GPSIMD:
-                nc.gpsimd.tensor_tensor(out=rec, in0=rec, in1=rec, op=ALU.mult)
+            rec = recs[:, b * C + c, :]
+            if (b, c) in V_UNITS:
+                nc.scalar.activation(out=rec, in_=rec, func=ACT.Abs_reciprocal_sqrt, bias=tiny2[:, 0:1], scale=1.0)
             else:
-                nc.scalar.activation(out=rec, in_=rec, func=ACT.Square)
-            rec_tiles[(b, c)] = rec
+                if (b, c) not in DC_ON_SCALAR:
+                    nc.scalar.activation(out=rec, in_=rec, func=ACT.Abs_reciprocal_sqrt, bias=tiny[:, 0:1], scale=1.0)
+                if (b, c) in G_UNITS:
+                    nc.gpsimd.tensor_tensor(out=rec, in0=rec, in1=rec, op=ALU.mult)
+                else:
+                    nc.scalar.activation(out=rec, in_=rec, func=ACT.Square)
 
         def normalise(b, c):
-            res = work.tile([P, G2], F32, name="res", tag="res", bufs=6)
+            res = work.tile([P, G2], F32, name="res", tag="res", bufs=5)
             for hh in range(HH):
                 cols = slice(hh * HW, (hh + 1) * HW)
                 nc.vector.scalar_tensor_tensor(
-                    out=res[:, cols], in0=rec_tiles[(b, c)][:, cols], scalar=1.0 / EPS,
+                    out=res[:, cols], in0=recs[:, b * C + c, cols], scalar=1.0 / EPS,
                     in1=banks[("a", b, c, hh)][:], op0=ALU.min, op1=ALU.mult,
                 )
-            nc.sync.dma_start(out=out[b, c], in_=res[:])
+                if (b, c) == (B - 1, C - 1):
+                    nc.sync.dma_start(out=out[b, c, :, cols], in_=res[:, cols])
+            if (b, c) != (B - 1, C - 1):
+                nc.sync.dma_start(out=out[b, c], in_=res[:])
 
-        kx_stage(0)
-        weights()
-        kx_stage(1)
-        kxb_stage(0)
-        left("m", 0, 0)
-        left("m", 0, 1)
-        qleft("m", 0, 0)
-        qleft("m", 0, 1)
-        ky_stage(0)
-        qy(0)
-        left("a", 0, 0)
-        ky_stage(1)
-        qy(1)
-        for c in range(4):
-            group("m", 0, c, 0)
-        left("a", 0, 1)
-        ky_stage(2)
-        qy(2)
-        for c in range(4):
-            dc(0, c, 0)
-            group("m", 0, c + 4, 0)
-        qleft("a", 0, 0)
-        ky_stage(3)
-        qy(3)
-        qleft("a", 0, 1)
-        for c in range(4):
-            dc(0, c + 4, 0)
-            group("m", 0, c, 1)
-        ky_stage(4)
-        qy(4)
-        for c in range(4):
-            dc(0, c, 1)
-            store_density(0, c)
-            group("m", 0, c + 4, 1)
-        for c in range(4, 6):
-            dc(0, c, 1)
-            store_density(0, c)
-        ky_stage(5)
-        qy(5)
-        for c in range(6, 8):
-            dc(0, c, 1)
-            store_density(0, c)
-        for c in range(2):
-            for hh in range(HH):
-                group("a", 0, c, hh)
-        kxb_stage(1)
-        left("m", 1, 0)
-        ky_stage(6)
-        qy(6)
-        left("m", 1, 1)
-        qleft("m", 1, 0)
-        ky_stage(7)
-        qy(7)
-        qleft("m", 1, 1)
-        for c in range(2):
-            for hh in range(HH):
-                group("m", 1, c, hh)
         def density_round(c):
             for hh in range(HH):
-                dc(1, c, hh)
+                density(1, c, hh)
                 if c + 2 < C:
                     group("m", 1, c + 2, hh)
-            store_density(1, c)
 
         def data_round(b, c):
             normalise(b, c)
@@ -290,8 +259,78 @@ def tile_convcnpweather_t_kernel(tc, x_lon, x_lat, wt, grid_lon, grid_lat, out):
                 for hh in range(HH):
                     group("a", nb, ncn, hh)
 
-        left("a", 1, 0)
-        left("a", 1, 1)
+        def mask_products(b):
+            left("m", b, 0, 0)
+            left("m", b, 0, 1)
+            qleft("m", b, 0, 0)
+            left("m", b, 1, 0)
+            qleft("m", b, 0, 1)
+            left("m", b, 1, 1)
+            qleft("m", b, 1, 0)
+            qleft("m", b, 1, 1)
+
+        kx_stage(0)
+        weights()
+        kx_stage(1)
+        kxb_stage(0)
+        left("a", 0, 1, 0)
+        left("a", 0, 1, 1)
+        left("a", 1, 0, 0)
+        left("a", 1, 0, 1)
+        mask_products(0)
+        ky_stage(0)
+        qy(0)
+        left("a", 0, 0, 0)
+        left("a", 0, 0, 1)
+        ky_stage(1)
+        qy(1)
+        kxb_stage(1)
+        for c in range(4):
+            group("m", 0, c, 0)
+        for c in range(4):
+            density(0, c, 0)
+            group("m", 0, c + 4, 0)
+        ky_stage(2)
+        qy(2)
+        for c in range(4, 8):
+            density(0, c, 0)
+        qleft("a", 0, 0, 0)
+        qleft("a", 0, 0, 1)
+        left("m", 1, 0, 0)
+        left("m", 1, 0, 1)
+        qleft("m", 1, 0, 0)
+        qleft("m", 1, 0, 1)
+        ky_stage(3)
+        qy(3)
+        for c in range(4):
+            group("m", 0, c, 1)
+        for c in range(4):
+            density(0, c, 1)
+            group("m", 0, c + 4, 1)
+        ky_stage(4)
+        qy(4)
+        for c in range(4, 8):
+            density(0, c, 1)
+        qleft("a", 0, 1, 0)
+        qleft("a", 0, 1, 1)
+        left("m", 1, 1, 0)
+        left("m", 1, 1, 1)
+        qleft("m", 1, 1, 0)
+        qleft("m", 1, 1, 1)
+        left("a", 1, 1, 0)
+        left("a", 1, 1, 1)
+        for c in range(2):
+            for hh in range(HH):
+                group("a", 0, c, hh)
+        ky_stage(5)
+        qy(5)
+        ky_stage(6)
+        qy(6)
+        ky_stage(7)
+        qy(7)
+        for c in range(2):
+            for hh in range(HH):
+                group("m", 1, c, hh)
         for c in range(C):
             recip(0, c)
         for c in range(4):
@@ -300,8 +339,9 @@ def tile_convcnpweather_t_kernel(tc, x_lon, x_lat, wt, grid_lon, grid_lat, out):
             data_round(0, c)
         for c in range(4, 8):
             density_round(c)
-        qleft("a", 1, 0)
-        qleft("a", 1, 1)
+        for k in range(KP):
+            for h in range(2):
+                qleft("a", 1, k, h)
         for c in range(4, 8):
             data_round(0, c)
         for c in range(C):

@@ -25,9 +25,10 @@ TINY2 = 1e-30
 FLOPS = 2 * B * (2 * C * G1) * N * G2
 
 V_UNITS = ()
-G_UNITS = ((1, 1), (1, 3), (1, 5), (1, 7))
-DC_ON_SCALAR = ()
-A_ON_VECTOR = ((0, 0, 0), (0, 0, 1), (1, 1, 1))
+G_UNITS = ((1, 0), (1, 2), (1, 4), (1, 6))
+DC_ON_SCALAR = ((1, 7),)
+A_ON_VECTOR = ((0, 0, 0), (0, 0, 1), (0, 1, 0), (0, 1, 1), (1, 1, 1))
+KX_SQUARES_ON_VECTOR = (1,)
 
 
 def tile_convcnpweather_t_kernel(tc, x_lon, x_lat, wt, grid_lon, grid_lat, out):
@@ -47,10 +48,11 @@ def tile_convcnpweather_t_kernel(tc, x_lon, x_lat, wt, grid_lon, grid_lat, out):
             nc.scalar.dma_start(out=glon[:], in_=grid_lon.partition_broadcast(P))
             nc.sync.dma_start(out=xs[:, 1], in_=x_lat.rearrange("b (k p t) -> p (b k) t", p=P, t=PACK))
             nc.scalar.dma_start(out=glat[:], in_=grid_lat.partition_broadcast(P))
-            nc.sync.dma_start(
-                out=wraw[:],
-                in_=wt.bitcast(I32).rearrange("b c (k p u) -> p (b c k) u", p=P, u=PACK // 2),
-            )
+            for b in range(B):
+                nc.sync.dma_start(
+                    out=wraw[:, b * C * KP : (b + 1) * C * KP, :],
+                    in_=wt.bitcast(I32)[b].rearrange("c (k p u) -> p (c k) u", p=P, u=PACK // 2),
+                )
 
         negx = keep.tile([P, 2, B * KP, PACK], F32, name="negx")
         tiny = keep.tile([P, 1], F32, name="tiny")
@@ -78,38 +80,52 @@ def tile_convcnpweather_t_kernel(tc, x_lon, x_lat, wt, grid_lon, grid_lat, out):
         y_scales = keep.tile([P, B * KP, G2], U8, name="y_scales", align_bytes=64)
         recs = keep.tile([P, B * C, G2], F32, name="recs")
 
-        def weights():
-            flat = "p b c k t -> p (b c k t)"
-            halves = wbits[:].rearrange("p b c k (u e) -> p (b c k u) e", e=2)
-            words = wraw[:].rearrange("p j u -> p (j u)")
+        def weights(b):
+            flat = "p c k t -> p (c k t)"
+            halves = wbits[:, b].rearrange("p c k (u e) -> p (c k u) e", e=2)
+            words = wraw[:, b * C * KP : (b + 1) * C * KP, :].rearrange("p j u -> p (j u)")
             nc.vector.tensor_scalar(
                 out=halves[:, :, 0], in0=words, scalar1=16, scalar2=None, op0=ALU.logical_shift_left
             )
             nc.vector.tensor_scalar(out=halves[:, :, 1], in0=words, scalar1=-65536, scalar2=None, op0=ALU.bitwise_and)
             nc.vector.tensor_scalar(
-                out=expo[:].rearrange(flat), in0=wbits[:].rearrange(flat), scalar1=23, scalar2=255,
+                out=expo[:, b].rearrange(flat), in0=wbits[:, b].rearrange(flat), scalar1=23, scalar2=255,
                 op0=ALU.logical_shift_right, op1=ALU.bitwise_and,
             )
             nc.vector.tensor_scalar(
-                out=maskb[:].rearrange(flat), in0=expo[:].rearrange(flat), scalar1=255.0, scalar2=None, op0=ALU.is_lt
+                out=maskb[:, b].rearrange(flat), in0=expo[:, b].rearrange(flat), scalar1=255.0, scalar2=None,
+                op0=ALU.is_lt,
             )
             nc.vector.tensor_scalar(
-                out=ones[:].rearrange(flat), in0=expo[:].rearrange(flat), scalar1=255.0, scalar2=-1.0,
+                out=ones[:, b].rearrange(flat), in0=expo[:, b].rearrange(flat), scalar1=255.0, scalar2=-1.0,
                 op0=ALU.is_lt, op1=ALU.mult,
             )
             nc.vector.tensor_tensor(
-                out=wkeep[:].rearrange(flat), in0=wbits[:].rearrange(flat), in1=ones[:].rearrange(flat),
+                out=wkeep[:, b].rearrange(flat), in0=wbits[:, b].rearrange(flat), in1=ones[:, b].rearrange(flat),
                 op=ALU.bitwise_and,
             )
 
         def kx_stage(b):
-            sqx = work.tile([P, KP, PACK, G1], F32, name="sqx", tag="sqx", bufs=1)
-            for k in range(KP):
-                for t in range(PACK):
-                    nc.scalar.activation(
-                        out=sqx[:, k, t, :], in_=glon[:], func=ACT.Square,
-                        bias=negx[:, 0, b * KP + k, t : t + 1], scale=1.0,
-                    )
+            sqx = work.tile([P, KP, PACK, G1], F32, name="sqx", tag="sqx", bufs=2)
+            if b in KX_SQUARES_ON_VECTOR:
+                dx = work.tile([P, KP * PACK, G1], F32, name="dx", tag="dx", bufs=1)
+                shift = negx[:, 0, b * KP : (b + 1) * KP, :].rearrange("p k t -> p (k t)")
+                nc.vector.tensor_tensor(
+                    out=dx[:],
+                    in0=glon[:].unsqueeze(1).to_broadcast([P, KP * PACK, G1]),
+                    in1=shift.unsqueeze(2).to_broadcast([P, KP * PACK, G1]),
+                    op=ALU.add,
+                )
+                nc.vector.tensor_tensor(
+                    out=sqx[:].rearrange("p k t g -> p (k t) g"), in0=dx[:], in1=dx[:], op=ALU.mult
+                )
+            else:
+                for k in range(KP):
+                    for t in range(PACK):
+                        nc.scalar.activation(
+                            out=sqx[:, k, t, :], in_=glon[:], func=ACT.Square,
+                            bias=negx[:, 0, b * KP + k, t : t + 1], scale=1.0,
+                        )
             nc.scalar.activation(
                 out=kx[:, b], in_=sqx[:].rearrange("p k t g -> p k g t"), func=ACT.Exp, scale=-GAMMA
             )
@@ -151,7 +167,7 @@ def tile_convcnpweather_t_kernel(tc, x_lon, x_lat, wt, grid_lon, grid_lat, out):
         def left(kind, b, k, h):
             c0 = h * CH
             if kind == "a":
-                prod = work.tile([P, CH, G1, PACK], BF16, name="prod_a", tag="prod_a", bufs=6, align_bytes=64)
+                prod = work.tile([P, CH, G1, PACK], BF16, name="prod_a", tag="prod_a", bufs=4, align_bytes=64)
                 step = CH if (b, k, h) in A_ON_VECTOR else 2
                 for c in range(0, CH, step):
                     eng = nc.vector if (b, k, h) in A_ON_VECTOR else nc.gpsimd
@@ -201,7 +217,7 @@ def tile_convcnpweather_t_kernel(tc, x_lon, x_lat, wt, grid_lon, grid_lat, out):
             cols = slice(hh * HW, (hh + 1) * HW)
             bank = banks[("m", b, c, hh)]
             if (b, c) in V_UNITS:
-                half = work.tile([P, HW], F32, name="half", tag="half", bufs=4)
+                half = work.tile([P, HW], F32, name="half", tag="half", bufs=2)
                 nc.vector.tensor_copy(out=half[:], in_=bank[:])
                 nc.vector.scalar_tensor_tensor(
                     out=recs[:, b * C + c, cols], in0=half[:], scalar=1.0, in1=bank[:], op0=ALU.mult, op1=ALU.mult
@@ -209,7 +225,7 @@ def tile_convcnpweather_t_kernel(tc, x_lon, x_lat, wt, grid_lon, grid_lat, out):
                 nc.sync.dma_start(out=out[b, C + c, :, cols], in_=half[:])
             else:
                 if (b, c) in DC_ON_SCALAR:
-                    half = work.tile([P, HW], F32, name="half", tag="half", bufs=4)
+                    half = work.tile([P, HW], F32, name="half", tag="half", bufs=2)
                     nc.scalar.copy(out=half[:], in_=bank[:])
                     nc.scalar.activation(
                         out=recs[:, b * C + c, cols], in_=bank[:], func=ACT.Abs_reciprocal_sqrt,
@@ -222,10 +238,12 @@ def tile_convcnpweather_t_kernel(tc, x_lon, x_lat, wt, grid_lon, grid_lat, out):
                         nc.sync.dma_start(out=out[b, C + c], in_=recs[:, b * C + c, :])
 
         def recip(b, c):
-            rec = recs[:, b * C + c, :]
-            if (b, c) in V_UNITS:
-                nc.scalar.activation(out=rec, in_=rec, func=ACT.Abs_reciprocal_sqrt, bias=tiny2[:, 0:1], scale=1.0)
-            else:
+            width = HW if (b, c) == (B - 1, C - 1) else G2
+            for lo in range(0, G2, width):
+                rec = recs[:, b * C + c, lo : lo + width]
+                if (b, c) in V_UNITS:
+                    nc.scalar.activation(out=rec, in_=rec, func=ACT.Abs_reciprocal_sqrt, bias=tiny2[:, 0:1], scale=1.0)
+                    continue
                 if (b, c) not in DC_ON_SCALAR:
                     nc.scalar.activation(out=rec, in_=rec, func=ACT.Abs_reciprocal_sqrt, bias=tiny[:, 0:1], scale=1.0)
                 if (b, c) in G_UNITS:
@@ -259,78 +277,69 @@ def tile_convcnpweather_t_kernel(tc, x_lon, x_lat, wt, grid_lon, grid_lat, out):
                 for hh in range(HH):
                     group("a", nb, ncn, hh)
 
-        def mask_products(b):
-            left("m", b, 0, 0)
-            left("m", b, 0, 1)
-            qleft("m", b, 0, 0)
-            left("m", b, 1, 0)
-            qleft("m", b, 0, 1)
-            left("m", b, 1, 1)
-            qleft("m", b, 1, 0)
-            qleft("m", b, 1, 1)
+        def both(step, kind, b, k):
+            step(kind, b, k, 0)
+            step(kind, b, k, 1)
 
         kx_stage(0)
-        weights()
         kx_stage(1)
+        weights(0)
         kxb_stage(0)
-        left("a", 0, 1, 0)
-        left("a", 0, 1, 1)
-        left("a", 1, 0, 0)
-        left("a", 1, 0, 1)
-        mask_products(0)
+        both(left, "m", 0, 0)
+        weights(1)
+        both(qleft, "m", 0, 0)
+        both(left, "m", 0, 1)
+        both(qleft, "m", 0, 1)
         ky_stage(0)
         qy(0)
-        left("a", 0, 0, 0)
-        left("a", 0, 0, 1)
+        both(left, "a", 0, 0)
         ky_stage(1)
         qy(1)
-        kxb_stage(1)
         for c in range(4):
             group("m", 0, c, 0)
+        both(left, "a", 0, 1)
+        ky_stage(2)
+        qy(2)
         for c in range(4):
             density(0, c, 0)
             group("m", 0, c + 4, 0)
-        ky_stage(2)
-        qy(2)
-        for c in range(4, 8):
-            density(0, c, 0)
-        qleft("a", 0, 0, 0)
-        qleft("a", 0, 0, 1)
-        left("m", 1, 0, 0)
-        left("m", 1, 0, 1)
-        qleft("m", 1, 0, 0)
-        qleft("m", 1, 0, 1)
+        both(qleft, "a", 0, 0)
         ky_stage(3)
         qy(3)
+        both(qleft, "a", 0, 1)
         for c in range(4):
+            density(0, c + 4, 0)
             group("m", 0, c, 1)
+        ky_stage(4)
+        qy(4)
         for c in range(4):
             density(0, c, 1)
             group("m", 0, c + 4, 1)
-        ky_stage(4)
-        qy(4)
-        for c in range(4, 8):
+        for c in range(4, 6):
             density(0, c, 1)
-        qleft("a", 0, 1, 0)
-        qleft("a", 0, 1, 1)
-        left("m", 1, 1, 0)
-        left("m", 1, 1, 1)
-        qleft("m", 1, 1, 0)
-        qleft("m", 1, 1, 1)
-        left("a", 1, 1, 0)
-        left("a", 1, 1, 1)
+        ky_stage(5)
+        qy(5)
+        for c in range(6, 8):
+            density(0, c, 1)
         for c in range(2):
             for hh in range(HH):
                 group("a", 0, c, hh)
-        ky_stage(5)
-        qy(5)
+        kxb_stage(1)
+        both(left, "m", 1, 0)
         ky_stage(6)
         qy(6)
+        both(qleft, "m", 1, 0)
+        both(left, "m", 1, 1)
         ky_stage(7)
         qy(7)
+        both(qleft, "m", 1, 1)
         for c in range(2):
             for hh in range(HH):
                 group("m", 1, c, hh)
+        left("a", 1, 1, 1)
+        left("a", 1, 0, 0)
+        left("a", 1, 0, 1)
+        left("a", 1, 1, 0)
         for c in range(C):
             recip(0, c)
         for c in range(4):
@@ -339,10 +348,11 @@ def tile_convcnpweather_t_kernel(tc, x_lon, x_lat, wt, grid_lon, grid_lat, out):
             data_round(0, c)
         for c in range(4, 8):
             density_round(c)
-        for k in range(KP):
-            for h in range(2):
-                qleft("a", 1, k, h)
-        for c in range(4, 8):
+        for c in range(4, 6):
+            data_round(0, c)
+        both(qleft, "a", 1, 0)
+        both(qleft, "a", 1, 1)
+        for c in range(6, 8):
             data_round(0, c)
         for c in range(C):
             recip(1, c)

@@ -26,8 +26,9 @@ FLOPS = 2 * B * (2 * C * G1) * N * G2
 
 V_UNITS = ()
 G_UNITS = ((1, 0), (1, 2), (1, 4), (1, 6))
-DC_ON_SCALAR = ((1, 7),)
-A_ON_VECTOR = ((0, 0, 0), (0, 0, 1), (0, 1, 0), (0, 1, 1), (1, 1, 1))
+DC_ON_SCALAR = ()
+A_ON_VECTOR = ((0, 0, 0), (0, 0, 1), (0, 1, 0), (0, 1, 1))
+PLAIN_COPY_ON_SCALAR = ()
 KX_SQUARES_ON_VECTOR = (1,)
 
 
@@ -37,7 +38,6 @@ def tile_convcnpweather_t_kernel(tc, x_lon, x_lat, wt, grid_lon, grid_lat, out):
         keep = ctx.enter_context(tc.tile_pool(name="keep", bufs=1))
         work = ctx.enter_context(tc.tile_pool(name="work", bufs=2))
         psum = ctx.enter_context(tc.psum_pool(name="psum", bufs=4))
-        ctx.enter_context(tc.manual_schedule())
 
         xs = keep.tile([P, 2, B * KP, PACK], BF16, name="xs")
         glon = keep.tile([P, G1], BF16, name="glon")
@@ -105,20 +105,20 @@ def tile_convcnpweather_t_kernel(tc, x_lon, x_lat, wt, grid_lon, grid_lat, out):
                 op=ALU.bitwise_and,
             )
 
-        def kx_stage(b):
+        sqx_tiles = {}
+
+        def kx_squares(b):
             sqx = work.tile([P, KP, PACK, G1], F32, name="sqx", tag="sqx", bufs=2)
             if b in KX_SQUARES_ON_VECTOR:
-                dx = work.tile([P, KP * PACK, G1], F32, name="dx", tag="dx", bufs=1)
+                flat = sqx[:].rearrange("p k t g -> p (k t) g")
                 shift = negx[:, 0, b * KP : (b + 1) * KP, :].rearrange("p k t -> p (k t)")
                 nc.vector.tensor_tensor(
-                    out=dx[:],
+                    out=flat,
                     in0=glon[:].unsqueeze(1).to_broadcast([P, KP * PACK, G1]),
                     in1=shift.unsqueeze(2).to_broadcast([P, KP * PACK, G1]),
                     op=ALU.add,
                 )
-                nc.vector.tensor_tensor(
-                    out=sqx[:].rearrange("p k t g -> p (k t) g"), in0=dx[:], in1=dx[:], op=ALU.mult
-                )
+                nc.vector.tensor_tensor(out=flat, in0=flat, in1=flat, op=ALU.mult)
             else:
                 for k in range(KP):
                     for t in range(PACK):
@@ -126,9 +126,13 @@ def tile_convcnpweather_t_kernel(tc, x_lon, x_lat, wt, grid_lon, grid_lat, out):
                             out=sqx[:, k, t, :], in_=glon[:], func=ACT.Square,
                             bias=negx[:, 0, b * KP + k, t : t + 1], scale=1.0,
                         )
-            nc.scalar.activation(
-                out=kx[:, b], in_=sqx[:].rearrange("p k t g -> p k g t"), func=ACT.Exp, scale=-GAMMA
-            )
+            sqx_tiles[b] = sqx
+
+        def kx_exp(b):
+            for k in range(KP):
+                nc.scalar.activation(
+                    out=kx[:, b, k], in_=sqx_tiles[b][:, k].rearrange("p t g -> p g t"), func=ACT.Exp, scale=-GAMMA
+                )
 
         def kxb_stage(b):
             nc.vector.tensor_copy(
@@ -137,14 +141,20 @@ def tile_convcnpweather_t_kernel(tc, x_lon, x_lat, wt, grid_lon, grid_lat, out):
 
         ky_tiles = {}
 
-        def ky_stage(r):
+        sq_tiles = {}
+
+        def ky_squares(r):
             b, hh, k = r // 4, (r // 2) % 2, r % 2
-            sq = work.tile([P, PACK, HW], F32, name="sq", tag="sq", bufs=1)
+            sq = work.tile([P, PACK, HW], F32, name="sq", tag="sq", bufs=3)
             for t in range(PACK):
                 nc.scalar.activation(
                     out=sq[:, t, :], in_=glat[:, hh * HW : (hh + 1) * HW], func=ACT.Square,
                     bias=negx[:, 1, b * KP + k, t : t + 1], scale=1.0,
                 )
+            sq_tiles[r] = sq
+
+        def ky_exp(r):
+            sq = sq_tiles[r]
             kyb = work.tile([P, HW, PACK], BF16, name="kyb", tag="kyb", bufs=3, align_bytes=64)
             nc.scalar.activation(
                 out=kyb[:].rearrange("p (c i) t -> p c t i", i=4),
@@ -167,7 +177,10 @@ def tile_convcnpweather_t_kernel(tc, x_lon, x_lat, wt, grid_lon, grid_lat, out):
         def left(kind, b, k, h):
             c0 = h * CH
             if kind == "a":
-                prod = work.tile([P, CH, G1, PACK], BF16, name="prod_a", tag="prod_a", bufs=4, align_bytes=64)
+                if (b, k, h) in A_ON_VECTOR:
+                    prod = work.tile([P, CH, G1, PACK], BF16, name="prod", tag="prod", bufs=6, align_bytes=64)
+                else:
+                    prod = work.tile([P, CH, G1, PACK], BF16, name="prod", tag="prod", bufs=6, align_bytes=64)
                 step = CH if (b, k, h) in A_ON_VECTOR else 2
                 for c in range(0, CH, step):
                     eng = nc.vector if (b, k, h) in A_ON_VECTOR else nc.gpsimd
@@ -178,7 +191,7 @@ def tile_convcnpweather_t_kernel(tc, x_lon, x_lat, wt, grid_lon, grid_lat, out):
                         op=ALU.mult,
                     )
             else:
-                prod = work.tile([P, CH, G1, PACK], BF16, name="prod_m", tag="prod_m", bufs=3, align_bytes=64)
+                prod = work.tile([P, CH, G1, PACK], BF16, name="prod", tag="prod", bufs=6, align_bytes=64)
                 nc.vector.tensor_tensor(
                     out=prod[:],
                     in0=kxb[:, b, k].unsqueeze(1).to_broadcast([P, CH, G1, PACK]),
@@ -217,7 +230,7 @@ def tile_convcnpweather_t_kernel(tc, x_lon, x_lat, wt, grid_lon, grid_lat, out):
             cols = slice(hh * HW, (hh + 1) * HW)
             bank = banks[("m", b, c, hh)]
             if (b, c) in V_UNITS:
-                half = work.tile([P, HW], F32, name="half", tag="half", bufs=2)
+                half = work.tile([P, HW], F32, name="half", tag="half", bufs=4)
                 nc.vector.tensor_copy(out=half[:], in_=bank[:])
                 nc.vector.scalar_tensor_tensor(
                     out=recs[:, b * C + c, cols], in0=half[:], scalar=1.0, in1=bank[:], op0=ALU.mult, op1=ALU.mult
@@ -225,7 +238,7 @@ def tile_convcnpweather_t_kernel(tc, x_lon, x_lat, wt, grid_lon, grid_lat, out):
                 nc.sync.dma_start(out=out[b, C + c, :, cols], in_=half[:])
             else:
                 if (b, c) in DC_ON_SCALAR:
-                    half = work.tile([P, HW], F32, name="half", tag="half", bufs=2)
+                    half = work.tile([P, HW], F32, name="half", tag="half", bufs=4)
                     nc.scalar.copy(out=half[:], in_=bank[:])
                     nc.scalar.activation(
                         out=recs[:, b * C + c, cols], in_=bank[:], func=ACT.Abs_reciprocal_sqrt,
@@ -233,26 +246,39 @@ def tile_convcnpweather_t_kernel(tc, x_lon, x_lat, wt, grid_lon, grid_lat, out):
                     )
                     nc.sync.dma_start(out=out[b, C + c, :, cols], in_=half[:])
                 else:
-                    nc.vector.tensor_copy(out=recs[:, b * C + c, cols], in_=bank[:])
+                    if (b, c) in PLAIN_COPY_ON_SCALAR:
+                        nc.scalar.copy(out=recs[:, b * C + c, cols], in_=bank[:])
+                    else:
+                        nc.vector.tensor_copy(out=recs[:, b * C + c, cols], in_=bank[:])
                     if hh == HH - 1:
                         nc.sync.dma_start(out=out[b, C + c], in_=recs[:, b * C + c, :])
 
-        def recip(b, c):
-            width = HW if (b, c) == (B - 1, C - 1) else G2
-            for lo in range(0, G2, width):
-                rec = recs[:, b * C + c, lo : lo + width]
-                if (b, c) in V_UNITS:
-                    nc.scalar.activation(out=rec, in_=rec, func=ACT.Abs_reciprocal_sqrt, bias=tiny2[:, 0:1], scale=1.0)
-                    continue
-                if (b, c) not in DC_ON_SCALAR:
-                    nc.scalar.activation(out=rec, in_=rec, func=ACT.Abs_reciprocal_sqrt, bias=tiny[:, 0:1], scale=1.0)
-                if (b, c) in G_UNITS:
-                    nc.gpsimd.tensor_tensor(out=rec, in0=rec, in1=rec, op=ALU.mult)
-                else:
-                    nc.scalar.activation(out=rec, in_=rec, func=ACT.Square)
+        def rsqrt(b, c, lo, width):
+            rec = recs[:, b * C + c, lo : lo + width]
+            if (b, c) in V_UNITS:
+                nc.scalar.activation(out=rec, in_=rec, func=ACT.Abs_reciprocal_sqrt, bias=tiny2[:, 0:1], scale=1.0)
+            elif (b, c) not in DC_ON_SCALAR:
+                nc.scalar.activation(out=rec, in_=rec, func=ACT.Abs_reciprocal_sqrt, bias=tiny[:, 0:1], scale=1.0)
+
+        def square(b, c, lo, width):
+            rec = recs[:, b * C + c, lo : lo + width]
+            if (b, c) in G_UNITS:
+                nc.gpsimd.tensor_tensor(out=rec, in0=rec, in1=rec, op=ALU.mult)
+            elif (b, c) not in V_UNITS:
+                nc.scalar.activation(out=rec, in_=rec, func=ACT.Square)
+
+        def recips(b):
+            parts = [(c, 0, G2) for c in range(C)]
+            if b == B - 1:
+                parts = parts[:-1] + [(C - 1, hh * HW, HW) for hh in range(HH)]
+            rsqrt(b, *parts[0])
+            for i in range(1, len(parts)):
+                rsqrt(b, *parts[i])
+                square(b, *parts[i - 1])
+            square(b, *parts[-1])
 
         def normalise(b, c):
-            res = work.tile([P, G2], F32, name="res", tag="res", bufs=5)
+            res = work.tile([P, G2], F32, name="res", tag="res", bufs=4)
             for hh in range(HH):
                 cols = slice(hh * HW, (hh + 1) * HW)
                 nc.vector.scalar_tensor_tensor(
@@ -281,8 +307,11 @@ def tile_convcnpweather_t_kernel(tc, x_lon, x_lat, wt, grid_lon, grid_lat, out):
             step(kind, b, k, 0)
             step(kind, b, k, 1)
 
-        kx_stage(0)
-        kx_stage(1)
+        kx_squares(0)
+        kx_squares(1)
+        kx_exp(0)
+        ky_squares(0)
+        kx_exp(1)
         weights(0)
         kxb_stage(0)
         both(left, "m", 0, 0)
@@ -290,34 +319,40 @@ def tile_convcnpweather_t_kernel(tc, x_lon, x_lat, wt, grid_lon, grid_lat, out):
         both(qleft, "m", 0, 0)
         both(left, "m", 0, 1)
         both(qleft, "m", 0, 1)
-        ky_stage(0)
+        ky_squares(1)
+        ky_exp(0)
         qy(0)
         both(left, "a", 0, 0)
-        ky_stage(1)
+        ky_squares(2)
+        ky_exp(1)
         qy(1)
         for c in range(4):
             group("m", 0, c, 0)
         both(left, "a", 0, 1)
-        ky_stage(2)
+        ky_squares(3)
+        ky_exp(2)
         qy(2)
         for c in range(4):
             density(0, c, 0)
             group("m", 0, c + 4, 0)
         both(qleft, "a", 0, 0)
-        ky_stage(3)
+        ky_squares(4)
+        ky_exp(3)
         qy(3)
         both(qleft, "a", 0, 1)
         for c in range(4):
             density(0, c + 4, 0)
             group("m", 0, c, 1)
-        ky_stage(4)
+        ky_squares(5)
+        ky_exp(4)
         qy(4)
         for c in range(4):
             density(0, c, 1)
             group("m", 0, c + 4, 1)
         for c in range(4, 6):
             density(0, c, 1)
-        ky_stage(5)
+        ky_squares(6)
+        ky_exp(5)
         qy(5)
         for c in range(6, 8):
             density(0, c, 1)
@@ -326,22 +361,22 @@ def tile_convcnpweather_t_kernel(tc, x_lon, x_lat, wt, grid_lon, grid_lat, out):
                 group("a", 0, c, hh)
         kxb_stage(1)
         both(left, "m", 1, 0)
-        ky_stage(6)
+        ky_squares(7)
+        ky_exp(6)
         qy(6)
         both(qleft, "m", 1, 0)
         both(left, "m", 1, 1)
-        ky_stage(7)
+        ky_exp(7)
         qy(7)
+        late = ky_tiles[7][:, 0, 0:1]
+        nc.vector.tensor_scalar(out=tiny[:], in0=late, scalar1=0.0, scalar2=TINY, op0=ALU.mult, op1=ALU.add)
         both(qleft, "m", 1, 1)
         for c in range(2):
             for hh in range(HH):
                 group("m", 1, c, hh)
-        left("a", 1, 1, 1)
-        left("a", 1, 0, 0)
-        left("a", 1, 0, 1)
-        left("a", 1, 1, 0)
-        for c in range(C):
-            recip(0, c)
+        both(left, "a", 1, 0)
+        both(left, "a", 1, 1)
+        recips(0)
         for c in range(4):
             density_round(c)
         for c in range(4):
@@ -354,7 +389,6 @@ def tile_convcnpweather_t_kernel(tc, x_lon, x_lat, wt, grid_lon, grid_lat, out):
         both(qleft, "a", 1, 1)
         for c in range(6, 8):
             data_round(0, c)
-        for c in range(C):
-            recip(1, c)
+        recips(1)
         for c in range(C):
             data_round(1, c)

@@ -43,16 +43,25 @@ def tile_convcnpweather_t_kernel(tc, x_lon, x_lat, wt, grid_lon, grid_lat, out):
         glon = keep.tile([P, G1], BF16, name="glon")
         glat = keep.tile([P, G2], BF16, name="glat")
         wraw = keep.tile([P, B * C * KP, PACK // 2], I32, name="wraw")
+        grow = keep.tile([P, G1 + G2], BF16, name="grow")
+        spread = keep.tile([P, P], BF16, name="spread")
+        nc.vector.memset(grow[:].bitcast(I32), 0)
+        nc.vector.memset(spread[:], 1.0)
+        nc.scalar.dma_start(out=grow[0:1, 0:G1], in_=grid_lon.rearrange("(o g) -> o g", o=1))
+        nc.scalar.dma_start(out=grow[0:1, G1:], in_=grid_lat.rearrange("(o g) -> o g", o=1))
         with nc.allow_non_contiguous_dma(reason="four neighbouring stations go to each partition"):
             nc.sync.dma_start(out=xs[:, 0], in_=x_lon.rearrange("b (k p t) -> p (b k) t", p=P, t=PACK))
-            nc.scalar.dma_start(out=glon[:], in_=grid_lon.partition_broadcast(P))
             nc.sync.dma_start(out=xs[:, 1], in_=x_lat.rearrange("b (k p t) -> p (b k) t", p=P, t=PACK))
-            nc.scalar.dma_start(out=glat[:], in_=grid_lat.partition_broadcast(P))
             for b in range(B):
                 nc.sync.dma_start(
                     out=wraw[:, b * C * KP : (b + 1) * C * KP, :],
                     in_=wt.bitcast(I32)[b].rearrange("c (k p u) -> p (c k) u", p=P, u=PACK // 2),
                 )
+
+        for dst, lo, width, used in ((glon[:], 0, 2 * G1, G1), (glat[:, 0:HW], G1, HW, HW), (glat[:, HW:], G1 + HW, HW, HW)):
+            rows = psum.tile([P, HW], F32, name="acc_a", tag="acc_a")
+            nc.tensor.matmul(out=rows[:, 0:width], lhsT=spread[:], rhs=grow[:, lo : lo + width], start=True, stop=True)
+            nc.vector.tensor_copy(out=dst, in_=rows[:, 0:used])
 
         negx = keep.tile([P, 2, B * KP, PACK], F32, name="negx")
         tiny = keep.tile([P, 1], F32, name="tiny")

@@ -18,18 +18,11 @@ KP = N // (P * PACK)
 HW = 512
 HH = G2 // HW
 CH = 4
+GC = 2
 GAMMA = 0.5 / (0.001 * 0.001)
 EPS = 1e-8
 TINY = 1e-18
-TINY2 = 1e-30
 FLOPS = 2 * B * (2 * C * G1) * N * G2
-
-V_UNITS = ()
-G_UNITS = ((1, 0), (1, 2), (1, 4), (1, 6))
-DC_ON_SCALAR = ()
-A_ON_VECTOR = ((0, 0, 0), (0, 0, 1), (0, 1, 0), (0, 1, 1))
-PLAIN_COPY_ON_SCALAR = ()
-KX_SQUARES_ON_VECTOR = (1,)
 
 
 def tile_convcnpweather_t_kernel(tc, x_lon, x_lat, wt, grid_lon, grid_lat, out):
@@ -39,17 +32,18 @@ def tile_convcnpweather_t_kernel(tc, x_lon, x_lat, wt, grid_lon, grid_lat, out):
         work = ctx.enter_context(tc.tile_pool(name="work", bufs=2))
         psum = ctx.enter_context(tc.psum_pool(name="psum", bufs=4))
 
+        lon_row = keep.tile([P, 2 * G1], BF16, name="lon_row")
+        lat_row = keep.tile([P, G2], BF16, name="lat_row")
+        ones = keep.tile([P, P], BF16, name="ones")
+        nc.vector.memset(lon_row[:].bitcast(I32), 0)
+        nc.vector.memset(ones[:], 1.0)
+        nc.vector.memset(lat_row[:].bitcast(I32), 0)
+        nc.scalar.dma_start(out=lon_row[0:1, 0:G1], in_=grid_lon.rearrange("(o g) -> o g", o=1))
+        nc.scalar.dma_start(out=lat_row[0:1, :], in_=grid_lat.rearrange("(o g) -> o g", o=1))
+
         xs = keep.tile([P, 2, B * KP, PACK], BF16, name="xs")
-        glon = keep.tile([P, G1], BF16, name="glon")
-        glat = keep.tile([P, G2], BF16, name="glat")
         wraw = keep.tile([P, B * C * KP, PACK // 2], I32, name="wraw")
-        grow = keep.tile([P, G1 + G2], BF16, name="grow")
-        spread = keep.tile([P, P], BF16, name="spread")
-        nc.vector.memset(grow[:].bitcast(I32), 0)
-        nc.vector.memset(spread[:], 1.0)
-        nc.scalar.dma_start(out=grow[0:1, 0:G1], in_=grid_lon.rearrange("(o g) -> o g", o=1))
-        nc.scalar.dma_start(out=grow[0:1, G1:], in_=grid_lat.rearrange("(o g) -> o g", o=1))
-        with nc.allow_non_contiguous_dma(reason="four neighbouring stations go to each partition"):
+        with nc.allow_non_contiguous_dma(reason="four neighbouring stations, 8 bytes, go to each partition"):
             nc.sync.dma_start(out=xs[:, 0], in_=x_lon.rearrange("b (k p t) -> p (b k) t", p=P, t=PACK))
             nc.sync.dma_start(out=xs[:, 1], in_=x_lat.rearrange("b (k p t) -> p (b k) t", p=P, t=PACK))
             for b in range(B):
@@ -58,28 +52,33 @@ def tile_convcnpweather_t_kernel(tc, x_lon, x_lat, wt, grid_lon, grid_lat, out):
                     in_=wt.bitcast(I32)[b].rearrange("c (k p u) -> p (c k) u", p=P, u=PACK // 2),
                 )
 
-        for dst, lo, width, used in ((glon[:], 0, 2 * G1, G1), (glat[:, 0:HW], G1, HW, HW), (glat[:, HW:], G1 + HW, HW, HW)):
-            rows = psum.tile([P, HW], F32, name="acc_a", tag="acc_a")
-            nc.tensor.matmul(out=rows[:, 0:width], lhsT=spread[:], rhs=grow[:, lo : lo + width], start=True, stop=True)
-            nc.vector.tensor_copy(out=dst, in_=rows[:, 0:used])
+        warm = keep.tile([P, 1], F32, name="warm")
+        nc.scalar.activation(out=warm[:], in_=ones[:, 0:1], func=ACT.Exp)
+
+        glon = keep.tile([P, G1], BF16, name="glon")
+        glat = keep.tile([P, G2], BF16, name="glat")
+        for dst, row, width in (
+            (glon[:], lon_row[:], G1),
+            (glat[:, 0:HW], lat_row[:, 0:HW], HW),
+            (glat[:, HW:], lat_row[:, HW:], HW),
+        ):
+            spread = psum.tile([P, HW], F32, name="acc_a", tag="acc_a")
+            cols = row.shape[1]
+            nc.tensor.matmul(out=spread[:, 0:cols], lhsT=ones[:], rhs=row, start=True, stop=True)
+            nc.vector.tensor_copy(out=dst, in_=spread[:, 0:width])
 
         negx = keep.tile([P, 2, B * KP, PACK], F32, name="negx")
-        tiny = keep.tile([P, 1], F32, name="tiny")
-        tiny2 = keep.tile([P, 1], F32, name="tiny2")
-        warm = keep.tile([P, 1], F32, name="warm")
-        nc.vector.memset(tiny[:], TINY)
-        nc.scalar.activation(out=warm[:], in_=tiny[:], func=ACT.Exp)
-        nc.vector.memset(tiny2[:], TINY2)
         nc.vector.tensor_scalar(out=negx[:], in0=xs[:], scalar1=-1.0, scalar2=None, op0=ALU.mult)
 
         kx = keep.tile([P, B, KP, G1, PACK], F32, name="kx")
         kxb = keep.tile([P, B, KP, G1, PACK], BF16, name="kxb")
         wbits = keep.tile([P, B, C, KP, PACK], I32, name="wbits")
         expo = keep.tile([P, B, C, KP, PACK], I32, name="expo")
-        ones = keep.tile([P, B, C, KP, PACK], I32, name="ones")
+        allset = keep.tile([P, B, C, KP, PACK], I32, name="allset")
         wkeep = keep.tile([P, B, C, KP, PACK], I32, name="wkeep")
         maskb = keep.tile([P, B, C, KP, PACK], BF16, name="maskb")
         wfin = wkeep[:].bitcast(F32)
+        tiny = keep.tile([P, 1], F32, name="tiny")
 
         a_codes = keep.tile([P, B * KP, C * G1], U32, name="a_codes", align_bytes=64)
         a_scales = keep.tile([P, B * KP, C * G1], U8, name="a_scales", align_bytes=64)
@@ -106,11 +105,11 @@ def tile_convcnpweather_t_kernel(tc, x_lon, x_lat, wt, grid_lon, grid_lat, out):
                 op0=ALU.is_lt,
             )
             nc.vector.tensor_scalar(
-                out=ones[:, b].rearrange(flat), in0=expo[:, b].rearrange(flat), scalar1=255.0, scalar2=-1.0,
+                out=allset[:, b].rearrange(flat), in0=expo[:, b].rearrange(flat), scalar1=255.0, scalar2=-1.0,
                 op0=ALU.is_lt, op1=ALU.mult,
             )
             nc.vector.tensor_tensor(
-                out=wkeep[:, b].rearrange(flat), in0=wbits[:, b].rearrange(flat), in1=ones[:, b].rearrange(flat),
+                out=wkeep[:, b].rearrange(flat), in0=wbits[:, b].rearrange(flat), in1=allset[:, b].rearrange(flat),
                 op=ALU.bitwise_and,
             )
 
@@ -118,7 +117,14 @@ def tile_convcnpweather_t_kernel(tc, x_lon, x_lat, wt, grid_lon, grid_lat, out):
 
         def kx_squares(b):
             sqx = work.tile([P, KP, PACK, G1], F32, name="sqx", tag="sqx", bufs=2)
-            if b in KX_SQUARES_ON_VECTOR:
+            if b == 0:
+                for k in range(KP):
+                    for t in range(PACK):
+                        nc.scalar.activation(
+                            out=sqx[:, k, t, :], in_=glon[:], func=ACT.Square,
+                            bias=negx[:, 0, b * KP + k, t : t + 1], scale=1.0,
+                        )
+            else:
                 flat = sqx[:].rearrange("p k t g -> p (k t) g")
                 shift = negx[:, 0, b * KP : (b + 1) * KP, :].rearrange("p k t -> p (k t)")
                 nc.vector.tensor_tensor(
@@ -128,13 +134,6 @@ def tile_convcnpweather_t_kernel(tc, x_lon, x_lat, wt, grid_lon, grid_lat, out):
                     op=ALU.add,
                 )
                 nc.vector.tensor_tensor(out=flat, in0=flat, in1=flat, op=ALU.mult)
-            else:
-                for k in range(KP):
-                    for t in range(PACK):
-                        nc.scalar.activation(
-                            out=sqx[:, k, t, :], in_=glon[:], func=ACT.Square,
-                            bias=negx[:, 0, b * KP + k, t : t + 1], scale=1.0,
-                        )
             sqx_tiles[b] = sqx
 
         def kx_exp(b):
@@ -143,17 +142,19 @@ def tile_convcnpweather_t_kernel(tc, x_lon, x_lat, wt, grid_lon, grid_lat, out):
                     out=kx[:, b, k], in_=sqx_tiles[b][:, k].rearrange("p t g -> p g t"), func=ACT.Exp, scale=-GAMMA
                 )
 
-        def kxb_stage(b):
+        def kx_round(b):
             nc.vector.tensor_copy(
                 out=kxb[:, b].rearrange("p k g t -> p (k g t)"), in_=kx[:, b].rearrange("p k g t -> p (k g t)")
             )
 
-        ky_tiles = {}
+        def chunk(r):
+            return r // (HH * KP), (r // KP) % HH, r % KP
 
         sq_tiles = {}
+        ky_tiles = {}
 
         def ky_squares(r):
-            b, hh, k = r // 4, (r // 2) % 2, r % 2
+            b, hh, k = chunk(r)
             sq = work.tile([P, PACK, HW], F32, name="sq", tag="sq", bufs=3)
             for t in range(PACK):
                 nc.scalar.activation(
@@ -163,17 +164,16 @@ def tile_convcnpweather_t_kernel(tc, x_lon, x_lat, wt, grid_lon, grid_lat, out):
             sq_tiles[r] = sq
 
         def ky_exp(r):
-            sq = sq_tiles[r]
             kyb = work.tile([P, HW, PACK], BF16, name="kyb", tag="kyb", bufs=3, align_bytes=64)
             nc.scalar.activation(
                 out=kyb[:].rearrange("p (c i) t -> p c t i", i=4),
-                in_=sq[:].rearrange("p t (c i) -> p c t i", i=4),
+                in_=sq_tiles[r][:].rearrange("p t (c i) -> p c t i", i=4),
                 func=ACT.Exp, scale=-GAMMA,
             )
             ky_tiles[r] = kyb
 
-        def qy(r):
-            b, hh, k = r // 4, (r // 2) % 2, r % 2
+        def ky_quantise(r):
+            b, hh, k = chunk(r)
             cols = slice(hh * HW, (hh + 1) * HW)
             nc.vector.quantize_mx(
                 out=y_codes[:, b * KP + k, cols].bitcast(FP8X4),
@@ -183,40 +183,30 @@ def tile_convcnpweather_t_kernel(tc, x_lon, x_lat, wt, grid_lon, grid_lat, out):
 
         lhs_tiles = {}
 
-        def left(kind, b, k, h):
-            c0 = h * CH
-            if kind == "a":
-                if (b, k, h) in A_ON_VECTOR:
-                    prod = work.tile([P, CH, G1, PACK], BF16, name="prod", tag="prod", bufs=6, align_bytes=64)
-                else:
-                    prod = work.tile([P, CH, G1, PACK], BF16, name="prod", tag="prod", bufs=6, align_bytes=64)
-                step = CH if (b, k, h) in A_ON_VECTOR else 2
+        def left(kind, b, k):
+            for h in range(C // CH):
+                prod = work.tile([P, CH, G1, PACK], BF16, name="prod", tag="prod", bufs=6, align_bytes=64)
+                engine, step = (nc.gpsimd, GC) if (kind, b) == ("a", 1) else (nc.vector, CH)
+                field, factor = (kx, wfin) if kind == "a" else (kxb, maskb)
                 for c in range(0, CH, step):
-                    eng = nc.vector if (b, k, h) in A_ON_VECTOR else nc.gpsimd
-                    eng.tensor_tensor(
+                    first = h * CH + c
+                    engine.tensor_tensor(
                         out=prod[:, c : c + step],
-                        in0=kx[:, b, k].unsqueeze(1).to_broadcast([P, step, G1, PACK]),
-                        in1=wfin[:, b, c0 + c : c0 + c + step, k, :].unsqueeze(2).to_broadcast([P, step, G1, PACK]),
+                        in0=field[:, b, k].unsqueeze(1).to_broadcast([P, step, G1, PACK]),
+                        in1=factor[:, b, first : first + step, k, :].unsqueeze(2).to_broadcast([P, step, G1, PACK]),
                         op=ALU.mult,
                     )
-            else:
-                prod = work.tile([P, CH, G1, PACK], BF16, name="prod", tag="prod", bufs=6, align_bytes=64)
-                nc.vector.tensor_tensor(
-                    out=prod[:],
-                    in0=kxb[:, b, k].unsqueeze(1).to_broadcast([P, CH, G1, PACK]),
-                    in1=maskb[:, b, c0 : c0 + CH, k, :].unsqueeze(2).to_broadcast([P, CH, G1, PACK]),
-                    op=ALU.mult,
-                )
-            lhs_tiles[(kind, b, k, h)] = prod
+                lhs_tiles[(kind, b, k, h)] = prod
 
-        def qleft(kind, b, k, h):
+        def left_quantise(kind, b, k):
             codes, scales = (a_codes, a_scales) if kind == "a" else (m_codes, m_scales)
-            cols = slice(h * CH * G1, (h + 1) * CH * G1)
-            nc.vector.quantize_mx(
-                out=codes[:, b * KP + k, cols].bitcast(FP8X4),
-                scales=scales[:, b * KP + k, cols],
-                in_=lhs_tiles[(kind, b, k, h)][:].rearrange("p c g t -> p (c g t)"),
-            )
+            for h in range(C // CH):
+                cols = slice(h * CH * G1, (h + 1) * CH * G1)
+                nc.vector.quantize_mx(
+                    out=codes[:, b * KP + k, cols].bitcast(FP8X4),
+                    scales=scales[:, b * KP + k, cols],
+                    in_=lhs_tiles[(kind, b, k, h)][:].rearrange("p c g t -> p (c g t)"),
+                )
 
         banks = {}
 
@@ -236,47 +226,22 @@ def tile_convcnpweather_t_kernel(tc, x_lon, x_lat, wt, grid_lon, grid_lat, out):
             banks[(kind, b, c, hh)] = acc
 
         def density(b, c, hh):
-            cols = slice(hh * HW, (hh + 1) * HW)
-            bank = banks[("m", b, c, hh)]
-            if (b, c) in V_UNITS:
-                half = work.tile([P, HW], F32, name="half", tag="half", bufs=4)
-                nc.vector.tensor_copy(out=half[:], in_=bank[:])
-                nc.vector.scalar_tensor_tensor(
-                    out=recs[:, b * C + c, cols], in0=half[:], scalar=1.0, in1=bank[:], op0=ALU.mult, op1=ALU.mult
-                )
-                nc.sync.dma_start(out=out[b, C + c, :, cols], in_=half[:])
-            else:
-                if (b, c) in DC_ON_SCALAR:
-                    half = work.tile([P, HW], F32, name="half", tag="half", bufs=4)
-                    nc.scalar.copy(out=half[:], in_=bank[:])
-                    nc.scalar.activation(
-                        out=recs[:, b * C + c, cols], in_=bank[:], func=ACT.Abs_reciprocal_sqrt,
-                        bias=tiny[:, 0:1], scale=1.0,
-                    )
-                    nc.sync.dma_start(out=out[b, C + c, :, cols], in_=half[:])
-                else:
-                    if (b, c) in PLAIN_COPY_ON_SCALAR:
-                        nc.scalar.copy(out=recs[:, b * C + c, cols], in_=bank[:])
-                    else:
-                        nc.vector.tensor_copy(out=recs[:, b * C + c, cols], in_=bank[:])
-                    if hh == HH - 1:
-                        nc.sync.dma_start(out=out[b, C + c], in_=recs[:, b * C + c, :])
+            nc.vector.tensor_copy(out=recs[:, b * C + c, hh * HW : (hh + 1) * HW], in_=banks[("m", b, c, hh)][:])
+            if hh == HH - 1:
+                nc.sync.dma_start(out=out[b, C + c], in_=recs[:, b * C + c, :])
 
         def rsqrt(b, c, lo, width):
             rec = recs[:, b * C + c, lo : lo + width]
-            if (b, c) in V_UNITS:
-                nc.scalar.activation(out=rec, in_=rec, func=ACT.Abs_reciprocal_sqrt, bias=tiny2[:, 0:1], scale=1.0)
-            elif (b, c) not in DC_ON_SCALAR:
-                nc.scalar.activation(out=rec, in_=rec, func=ACT.Abs_reciprocal_sqrt, bias=tiny[:, 0:1], scale=1.0)
+            nc.scalar.activation(out=rec, in_=rec, func=ACT.Abs_reciprocal_sqrt, bias=tiny[:, 0:1], scale=1.0)
 
         def square(b, c, lo, width):
             rec = recs[:, b * C + c, lo : lo + width]
-            if (b, c) in G_UNITS:
+            if b == 1 and c % 2 == 0:
                 nc.gpsimd.tensor_tensor(out=rec, in0=rec, in1=rec, op=ALU.mult)
-            elif (b, c) not in V_UNITS:
+            else:
                 nc.scalar.activation(out=rec, in_=rec, func=ACT.Square)
 
-        def recips(b):
+        def reciprocals(b):
             parts = [(c, 0, G2) for c in range(C)]
             if b == B - 1:
                 parts = parts[:-1] + [(C - 1, hh * HW, HW) for hh in range(HH)]
@@ -287,6 +252,7 @@ def tile_convcnpweather_t_kernel(tc, x_lon, x_lat, wt, grid_lon, grid_lat, out):
             square(b, *parts[-1])
 
         def normalise(b, c):
+            last = (b, c) == (B - 1, C - 1)
             res = work.tile([P, G2], F32, name="res", tag="res", bufs=4)
             for hh in range(HH):
                 cols = slice(hh * HW, (hh + 1) * HW)
@@ -294,9 +260,9 @@ def tile_convcnpweather_t_kernel(tc, x_lon, x_lat, wt, grid_lon, grid_lat, out):
                     out=res[:, cols], in0=recs[:, b * C + c, cols], scalar=1.0 / EPS,
                     in1=banks[("a", b, c, hh)][:], op0=ALU.min, op1=ALU.mult,
                 )
-                if (b, c) == (B - 1, C - 1):
+                if last:
                     nc.sync.dma_start(out=out[b, c, :, cols], in_=res[:, cols])
-            if (b, c) != (B - 1, C - 1):
+            if not last:
                 nc.sync.dma_start(out=out[b, c], in_=res[:])
 
         def density_round(c):
@@ -307,14 +273,16 @@ def tile_convcnpweather_t_kernel(tc, x_lon, x_lat, wt, grid_lon, grid_lat, out):
 
         def data_round(b, c):
             normalise(b, c)
-            nb, ncn = (b, c + 2) if c + 2 < C else (b + 1, c + 2 - C)
+            nb, nxt = (b, c + 2) if c + 2 < C else (b + 1, c + 2 - C)
             if nb < B:
                 for hh in range(HH):
-                    group("a", nb, ncn, hh)
+                    group("a", nb, nxt, hh)
 
-        def both(step, kind, b, k):
-            step(kind, b, k, 0)
-            step(kind, b, k, 1)
+        def ky_step(r):
+            if r + 1 < B * HH * KP:
+                ky_squares(r + 1)
+            ky_exp(r)
+            ky_quantise(r)
 
         kx_squares(0)
         kx_squares(1)
@@ -322,70 +290,56 @@ def tile_convcnpweather_t_kernel(tc, x_lon, x_lat, wt, grid_lon, grid_lat, out):
         ky_squares(0)
         kx_exp(1)
         weights(0)
-        kxb_stage(0)
-        both(left, "m", 0, 0)
+        kx_round(0)
+        left("m", 0, 0)
         weights(1)
-        both(qleft, "m", 0, 0)
-        both(left, "m", 0, 1)
-        both(qleft, "m", 0, 1)
-        ky_squares(1)
-        ky_exp(0)
-        qy(0)
-        both(left, "a", 0, 0)
-        ky_squares(2)
-        ky_exp(1)
-        qy(1)
+        left_quantise("m", 0, 0)
+        left("m", 0, 1)
+        left_quantise("m", 0, 1)
+        ky_step(0)
+        left("a", 0, 0)
+        ky_step(1)
         for c in range(4):
             group("m", 0, c, 0)
-        both(left, "a", 0, 1)
-        ky_squares(3)
-        ky_exp(2)
-        qy(2)
+        left("a", 0, 1)
+        ky_step(2)
         for c in range(4):
             density(0, c, 0)
             group("m", 0, c + 4, 0)
-        both(qleft, "a", 0, 0)
-        ky_squares(4)
-        ky_exp(3)
-        qy(3)
-        both(qleft, "a", 0, 1)
+        left_quantise("a", 0, 0)
+        ky_step(3)
+        left_quantise("a", 0, 1)
         for c in range(4):
             density(0, c + 4, 0)
             group("m", 0, c, 1)
-        ky_squares(5)
-        ky_exp(4)
-        qy(4)
+        ky_step(4)
         for c in range(4):
             density(0, c, 1)
             group("m", 0, c + 4, 1)
         for c in range(4, 6):
             density(0, c, 1)
-        ky_squares(6)
-        ky_exp(5)
-        qy(5)
+        ky_step(5)
         for c in range(6, 8):
             density(0, c, 1)
         for c in range(2):
             for hh in range(HH):
                 group("a", 0, c, hh)
-        kxb_stage(1)
-        both(left, "m", 1, 0)
-        ky_squares(7)
-        ky_exp(6)
-        qy(6)
-        both(qleft, "m", 1, 0)
-        both(left, "m", 1, 1)
-        ky_exp(7)
-        qy(7)
-        late = ky_tiles[7][:, 0, 0:1]
-        nc.vector.tensor_scalar(out=tiny[:], in0=late, scalar1=0.0, scalar2=TINY, op0=ALU.mult, op1=ALU.add)
-        both(qleft, "m", 1, 1)
+        kx_round(1)
+        left("m", 1, 0)
+        ky_step(6)
+        left_quantise("m", 1, 0)
+        left("m", 1, 1)
+        ky_step(7)
+        nc.vector.tensor_scalar(
+            out=tiny[:], in0=ky_tiles[B * HH * KP - 1][:, 0, 0:1], scalar1=0.0, scalar2=TINY, op0=ALU.mult, op1=ALU.add
+        )
+        left_quantise("m", 1, 1)
         for c in range(2):
             for hh in range(HH):
                 group("m", 1, c, hh)
-        both(left, "a", 1, 0)
-        both(left, "a", 1, 1)
-        recips(0)
+        left("a", 1, 0)
+        left("a", 1, 1)
+        reciprocals(0)
         for c in range(4):
             density_round(c)
         for c in range(4):
@@ -394,10 +348,10 @@ def tile_convcnpweather_t_kernel(tc, x_lon, x_lat, wt, grid_lon, grid_lat, out):
             density_round(c)
         for c in range(4, 6):
             data_round(0, c)
-        both(qleft, "a", 1, 0)
-        both(qleft, "a", 1, 1)
+        left_quantise("a", 1, 0)
+        left_quantise("a", 1, 1)
         for c in range(6, 8):
             data_round(0, c)
-        recips(1)
+        reciprocals(1)
         for c in range(C):
             data_round(1, c)

@@ -55,20 +55,17 @@ def tile_convcnpweather_t_kernel(tc, x_lon, x_lat, wt, grid_lon, grid_lat, out):
         warm = keep.tile([P, 1], F32, name="warm")
         nc.scalar.activation(out=warm[:], in_=ones[:, 0:1], func=ACT.Exp)
 
-        glon = keep.tile([P, G1], BF16, name="glon")
-        glat = keep.tile([P, G2], BF16, name="glat")
-        for dst, row, width in (
-            (glon[:], lon_row[:], G1),
-            (glat[:, 0:HW], lat_row[:, 0:HW], HW),
-            (glat[:, HW:], lat_row[:, HW:], HW),
-        ):
+        glon = []
+        for b in range(B):
             spread = psum.tile([P, HW], F32, name="acc_a", tag="acc_a")
-            cols = row.shape[1]
-            nc.tensor.matmul(out=spread[:, 0:cols], lhsT=ones[:], rhs=row, start=True, stop=True)
-            nc.vector.tensor_copy(out=dst, in_=spread[:, 0:width])
-
-        negx = keep.tile([P, 2, B * KP, PACK], F32, name="negx")
-        nc.vector.tensor_scalar(out=negx[:], in0=xs[:], scalar1=-1.0, scalar2=None, op0=ALU.mult)
+            nc.tensor.matmul(out=spread[:, 0 : 2 * G1], lhsT=ones[:], rhs=lon_row[:], start=True, stop=True)
+            glon.append(spread[:, 0:G1])
+        glat = keep.tile([P, G2], BF16, name="glat")
+        for hh in range(HH):
+            cols = slice(hh * HW, (hh + 1) * HW)
+            spread = psum.tile([P, HW], F32, name="acc_a", tag="acc_a")
+            nc.tensor.matmul(out=spread[:], lhsT=ones[:], rhs=lat_row[:, cols], start=True, stop=True)
+            nc.vector.tensor_copy(out=glat[:, cols], in_=spread[:])
 
         kx = keep.tile([P, B, KP, G1, PACK], F32, name="kx")
         kxb = keep.tile([P, B, KP, G1, PACK], BF16, name="kxb")
@@ -121,17 +118,17 @@ def tile_convcnpweather_t_kernel(tc, x_lon, x_lat, wt, grid_lon, grid_lat, out):
                 for k in range(KP):
                     for t in range(PACK):
                         nc.scalar.activation(
-                            out=sqx[:, k, t, :], in_=glon[:], func=ACT.Square,
-                            bias=negx[:, 0, b * KP + k, t : t + 1], scale=1.0,
+                            out=sqx[:, k, t, :], in_=glon[b], func=ACT.Square,
+                            bias=xs[:, 0, b * KP + k, t : t + 1], scale=-1.0,
                         )
             else:
                 flat = sqx[:].rearrange("p k t g -> p (k t) g")
-                shift = negx[:, 0, b * KP : (b + 1) * KP, :].rearrange("p k t -> p (k t)")
+                here = xs[:, 0, b * KP : (b + 1) * KP, :].rearrange("p k t -> p (k t)")
                 nc.vector.tensor_tensor(
                     out=flat,
-                    in0=glon[:].unsqueeze(1).to_broadcast([P, KP * PACK, G1]),
-                    in1=shift.unsqueeze(2).to_broadcast([P, KP * PACK, G1]),
-                    op=ALU.add,
+                    in0=glon[b].unsqueeze(1).to_broadcast([P, KP * PACK, G1]),
+                    in1=here.unsqueeze(2).to_broadcast([P, KP * PACK, G1]),
+                    op=ALU.subtract,
                 )
                 nc.vector.tensor_tensor(out=flat, in0=flat, in1=flat, op=ALU.mult)
             sqx_tiles[b] = sqx
@@ -159,7 +156,7 @@ def tile_convcnpweather_t_kernel(tc, x_lon, x_lat, wt, grid_lon, grid_lat, out):
             for t in range(PACK):
                 nc.scalar.activation(
                     out=sq[:, t, :], in_=glat[:, hh * HW : (hh + 1) * HW], func=ACT.Square,
-                    bias=negx[:, 1, b * KP + k, t : t + 1], scale=1.0,
+                    bias=xs[:, 1, b * KP + k, t : t + 1], scale=-1.0,
                 )
             sq_tiles[r] = sq
 
@@ -226,7 +223,11 @@ def tile_convcnpweather_t_kernel(tc, x_lon, x_lat, wt, grid_lon, grid_lat, out):
             banks[(kind, b, c, hh)] = acc
 
         def density(b, c, hh):
-            nc.vector.tensor_copy(out=recs[:, b * C + c, hh * HW : (hh + 1) * HW], in_=banks[("m", b, c, hh)][:])
+            dst = recs[:, b * C + c, hh * HW : (hh + 1) * HW]
+            if b == 1 and c % 4 == 1:
+                nc.scalar.copy(out=dst, in_=banks[("m", b, c, hh)][:])
+            else:
+                nc.vector.tensor_copy(out=dst, in_=banks[("m", b, c, hh)][:])
             if hh == HH - 1:
                 nc.sync.dma_start(out=out[b, C + c], in_=recs[:, b * C + c, :])
 
@@ -236,7 +237,7 @@ def tile_convcnpweather_t_kernel(tc, x_lon, x_lat, wt, grid_lon, grid_lat, out):
 
         def square(b, c, lo, width):
             rec = recs[:, b * C + c, lo : lo + width]
-            if b == 1 and c % 2 == 0:
+            if (b + c) % 2 == 1:
                 nc.gpsimd.tensor_tensor(out=rec, in0=rec, in1=rec, op=ALU.mult)
             else:
                 nc.scalar.activation(out=rec, in_=rec, func=ACT.Square)

from contextlib import ExitStack

import concourse.mybir as mybir

F32 = mybir.dt.float32
BF16 = mybir.dt.bfloat16
U32 = mybir.dt.uint32
U8 = mybir.dt.uint8
I32 = mybir.dt.int32
FP8X4 = mybir.dt.float8_e4m3fn_x4
ACT = mybir.ActivationFunctionType
ALU = mybir.AluOpType

P = 128
B, C, N, G1, G2 = 2, 8, 1024, 128, 1024
PACK = 4
KP = N // (P * PACK)
HW = 512
HH = G2 // HW
CH = 4
GC = 2
GAMMA = 0.5 / (0.001 * 0.001)
EPS = 1e-8
TINY = 1e-18
FLOPS = 2 * B * (2 * C * G1) * N * G2


def tile_convcnpweather_t_kernel(tc, x_lon, x_lat, wt, grid_lon, grid_lat, out):
    nc = tc.nc
    with ExitStack() as ctx:
        keep = ctx.enter_context(tc.tile_pool(name="keep", bufs=1))
        work = ctx.enter_context(tc.tile_pool(name="work", bufs=2))
        psum = ctx.enter_context(tc.psum_pool(name="psum", bufs=4))

        lon_row = keep.tile([P, 2 * G1], BF16, name="lon_row")
        lat_row = keep.tile([P, G2], BF16, name="lat_row")
        ones = keep.tile([P, P], BF16, name="ones")
        nc.vector.memset(lon_row[:].bitcast(I32), 0)
        nc.vector.memset(ones[:], 1.0)
        nc.vector.memset(lat_row[:].bitcast(I32), 0)
        nc.scalar.dma_start(out=lon_row[0:1, 0:G1], in_=grid_lon.rearrange("(o g) -> o g", o=1))
        nc.scalar.dma_start(out=lat_row[0:1, :], in_=grid_lat.rearrange("(o g) -> o g", o=1))

        xs = keep.tile([P, 2, B * KP, PACK], BF16, name="xs")
        wraw = keep.tile([P, B * C * KP, PACK // 2], I32, name="wraw")
        with nc.allow_non_contiguous_dma(reason="four neighbouring stations, 8 bytes, go to each partition"):
            nc.sync.dma_start(out=xs[:, 0], in_=x_lon.rearrange("b (k p t) -> p (b k) t", p=P, t=PACK))
            nc.sync.dma_start(out=xs[:, 1], in_=x_lat.rearrange("b (k p t) -> p (b k) t", p=P, t=PACK))
            for b in range(B):
                nc.sync.dma_start(
                    out=wraw[:, b * C * KP : (b + 1) * C * KP, :],
                    in_=wt.bitcast(I32)[b].rearrange("c (k p u) -> p (c k) u", p=P, u=PACK // 2),
                )

        warm = keep.tile([P, 1], F32, name="warm")
        nc.scalar.activation(out=warm[:], in_=ones[:, 0:1], func=ACT.Exp)

        glon = []
        for b in range(B):
            spread = psum.tile([P, HW], F32, name="acc_a", tag="acc_a")
            nc.tensor.matmul(out=spread[:, 0 : 2 * G1], lhsT=ones[:], rhs=lon_row[:], start=True, stop=True)
            glon.append(spread[:, 0:G1])
        glat = keep.tile([P, G2], BF16, name="glat")
        for hh in range(HH):
            cols = slice(hh * HW, (hh + 1) * HW)
            spread = psum.tile([P, HW], F32, name="acc_a", tag="acc_a")
            nc.tensor.matmul(out=spread[:], lhsT=ones[:], rhs=lat_row[:, cols], start=True, stop=True)
            nc.vector.tensor_copy(out=glat[:, cols], in_=spread[:])

        kx = keep.tile([P, B, KP, G1, PACK], F32, name="kx")
        kxb = keep.tile([P, B, KP, G1, PACK], BF16, name="kxb")
        wbits = keep.tile([P, B, C, KP, PACK], I32, name="wbits")
        expo = keep.tile([P, B, C, KP, PACK], I32, name="expo")
        allset = keep.tile([P, B, C, KP, PACK], I32, name="allset")
        wkeep = keep.tile([P, B, C, KP, PACK], I32, name="wkeep")
        maskb = keep.tile([P, B, C, KP, PACK], BF16, name="maskb")
        wfin = wkeep[:].bitcast(F32)
        tiny = keep.tile([P, 1], F32, name="tiny")

        a_codes = keep.tile([P, B * KP, C * G1], U32, name="a_codes", align_bytes=64)
        a_scales = keep.tile([P, B * KP, C * G1], U8, name="a_scales", align_bytes=64)
        m_codes = keep.tile([P, B * KP, C * G1], U32, name="m_codes", align_bytes=64)
        m_scales = keep.tile([P, B * KP, C * G1], U8, name="m_scales", align_bytes=64)
        y_codes = keep.tile([P, B * KP, G2], U32, name="y_codes", align_bytes=64)
        y_scales = keep.tile([P, B * KP, G2], U8, name="y_scales", align_bytes=64)
        recs = keep.tile([P, B * C, G2], F32, name="recs")

        def weights(b):
            flat = "p c k t -> p (c k t)"
            halves = wbits[:, b].rearrange("p c k (u e) -> p (c k u) e", e=2)
            words = wraw[:, b * C * KP : (b + 1) * C * KP, :].rearrange("p j u -> p (j u)")
            nc.vector.tensor_scalar(
                out=halves[:, :, 0], in0=words, scalar1=16, scalar2=None, op0=ALU.logical_shift_left
            )
            nc.vector.tensor_scalar(out=halves[:, :, 1], in0=words, scalar1=-65536, scalar2=None, op0=ALU.bitwise_and)
            nc.vector.tensor_scalar(
                out=expo[:, b].rearrange(flat), in0=wbits[:, b].rearrange(flat), scalar1=23, scalar2=255,
                op0=ALU.logical_shift_right, op1=ALU.bitwise_and,
            )
            nc.vector.tensor_scalar(
                out=maskb[:, b].rearrange(flat), in0=expo[:, b].rearrange(flat), scalar1=255.0, scalar2=None,
                op0=ALU.is_lt,
            )
            nc.vector.tensor_scalar(
                out=allset[:, b].rearrange(flat), in0=expo[:, b].rearrange(flat), scalar1=255.0, scalar2=-1.0,
                op0=ALU.is_lt, op1=ALU.mult,
            )
            nc.vector.tensor_tensor(
                out=wkeep[:, b].rearrange(flat), in0=wbits[:, b].rearrange(flat), in1=allset[:, b].rearrange(flat),
                op=ALU.bitwise_and,
            )

        sqx_tiles = {}

        def kx_squares(b):
            sqx = work.tile([P, KP, PACK, G1], F32, name="sqx", tag="sqx", bufs=2)
            if b == 0:
                for k in range(KP):
                    for t in range(PACK):
                        nc.scalar.activation(
                            out=sqx[:, k, t, :], in_=glon[b], func=ACT.Square,
                            bias=xs[:, 0, b * KP + k, t : t + 1], scale=-1.0,
                        )
            else:
                flat = sqx[:].rearrange("p k t g -> p (k t) g")
                here = xs[:, 0, b * KP : (b + 1) * KP, :].rearrange("p k t -> p (k t)")
                nc.vector.tensor_tensor(
                    out=flat,
                    in0=glon[b].unsqueeze(1).to_broadcast([P, KP * PACK, G1]),
                    in1=here.unsqueeze(2).to_broadcast([P, KP * PACK, G1]),
                    op=ALU.subtract,
                )
                nc.vector.tensor_tensor(out=flat, in0=flat, in1=flat, op=ALU.mult)
            sqx_tiles[b] = sqx

        def kx_exp(b):
            for k in range(KP):
                nc.scalar.activation(
                    out=kx[:, b, k], in_=sqx_tiles[b][:, k].rearrange("p t g -> p g t"), func=ACT.Exp, scale=-GAMMA
                )

        def kx_round(b):
            nc.vector.tensor_copy(
                out=kxb[:, b].rearrange("p k g t -> p (k g t)"), in_=kx[:, b].rearrange("p k g t -> p (k g t)")
            )

        def chunk(r):
            return r // (HH * KP), (r // KP) % HH, r % KP

        sq_tiles = {}
        ky_tiles = {}

        def ky_squares(r):
            b, hh, k = chunk(r)
            sq = work.tile([P, PACK, HW], F32, name="sq", tag="sq", bufs=3)
            for t in range(PACK):
                nc.scalar.activation(
                    out=sq[:, t, :], in_=glat[:, hh * HW : (hh + 1) * HW], func=ACT.Square,
                    bias=xs[:, 1, b * KP + k, t : t + 1], scale=-1.0,
                )
            sq_tiles[r] = sq

        def ky_exp(r):
            kyb = work.tile([P, HW, PACK], BF16, name="kyb", tag="kyb", bufs=3, align_bytes=64)
            nc.scalar.activation(
                out=kyb[:].rearrange("p (c i) t -> p c t i", i=4),
                in_=sq_tiles[r][:].rearrange("p t (c i) -> p c t i", i=4),
                func=ACT.Exp, scale=-GAMMA,
            )
            ky_tiles[r] = kyb

        def ky_quantise(r):
            b, hh, k = chunk(r)
            cols = slice(hh * HW, (hh + 1) * HW)
            nc.vector.quantize_mx(
                out=y_codes[:, b * KP + k, cols].bitcast(FP8X4),
                scales=y_scales[:, b * KP + k, cols],
                in_=ky_tiles[r][:].rearrange("p h t -> p (h t)"),
            )

        lhs_tiles = {}

        def left(kind, b, k):
            for h in range(C // CH):
                prod = work.tile([P, CH, G1, PACK], BF16, name="prod", tag="prod", bufs=6, align_bytes=64)
                engine, step = (nc.gpsimd, GC) if (kind, b) == ("a", 1) else (nc.vector, CH)
                field, factor = (kx, wfin) if kind == "a" else (kxb, maskb)
                for c in range(0, CH, step):
                    first = h * CH + c
                    engine.tensor_tensor(
                        out=prod[:, c : c + step],
                        in0=field[:, b, k].unsqueeze(1).to_broadcast([P, step, G1, PACK]),
                        in1=factor[:, b, first : first + step, k, :].unsqueeze(2).to_broadcast([P, step, G1, PACK]),
                        op=ALU.mult,
                    )
                lhs_tiles[(kind, b, k, h)] = prod

        def left_quantise(kind, b, k):
            codes, scales = (a_codes, a_scales) if kind == "a" else (m_codes, m_scales)
            for h in range(C // CH):
                cols = slice(h * CH * G1, (h + 1) * CH * G1)
                nc.vector.quantize_mx(
                    out=codes[:, b * KP + k, cols].bitcast(FP8X4),
                    scales=scales[:, b * KP + k, cols],
                    in_=lhs_tiles[(kind, b, k, h)][:].rearrange("p c g t -> p (c g t)"),
                )

        banks = {}

        def group(kind, b, c, hh):
            codes, scales = (a_codes, a_scales) if kind == "a" else (m_codes, m_scales)
            acc = psum.tile([P, HW], F32, name="acc_" + kind, tag="acc_" + kind)
            for k in range(KP):
                nc.tensor.matmul_mx(
                    out=acc[:],
                    lhsT=codes[:, b * KP + k, c * G1 : (c + 1) * G1].bitcast(FP8X4),
                    lhsT_scale=scales[:, b * KP + k, c * G1 : (c + 1) * G1],
                    rhs=y_codes[:, b * KP + k, hh * HW : (hh + 1) * HW].bitcast(FP8X4),
                    rhs_scale=y_scales[:, b * KP + k, hh * HW : (hh + 1) * HW],
                    start=(k == 0),
                    stop=(k == KP - 1),
                )
            banks[(kind, b, c, hh)] = acc

        def density(b, c, hh):
            dst = recs[:, b * C + c, hh * HW : (hh + 1) * HW]
            if b == 1 and c % 4 == 1:
                nc.scalar.copy(out=dst, in_=banks[("m", b, c, hh)][:])
            else:
                nc.vector.tensor_copy(out=dst, in_=banks[("m", b, c, hh)][:])
            if hh == HH - 1:
                nc.sync.dma_start(out=out[b, C + c], in_=recs[:, b * C + c, :])

        def rsqrt(b, c, lo, width):
            rec = recs[:, b * C + c, lo : lo + width]
            nc.scalar.activation(out=rec, in_=rec, func=ACT.Abs_reciprocal_sqrt, bias=tiny[:, 0:1], scale=1.0)

        def square(b, c, lo, width):
            rec = recs[:, b * C + c, lo : lo + width]
            if (b + c) % 2 == 1:
                nc.gpsimd.tensor_tensor(out=rec, in0=rec, in1=rec, op=ALU.mult)
            else:
                nc.scalar.activation(out=rec, in_=rec, func=ACT.Square)

        def reciprocals(b):
            parts = [(c, 0, G2) for c in range(C)]
            if b == B - 1:
                parts = parts[:-1] + [(C - 1, hh * HW, HW) for hh in range(HH)]
            rsqrt(b, *parts[0])
            for i in range(1, len(parts)):
                rsqrt(b, *parts[i])
                square(b, *parts[i - 1])
            square(b, *parts[-1])

        def normalise(b, c):
            last = (b, c) == (B - 1, C - 1)
            res = work.tile([P, G2], F32, name="res", tag="res", bufs=4)
            for hh in range(HH):
                cols = slice(hh * HW, (hh + 1) * HW)
                nc.vector.scalar_tensor_tensor(
                    out=res[:, cols], in0=recs[:, b * C + c, cols], scalar=1.0 / EPS,
                    in1=banks[("a", b, c, hh)][:], op0=ALU.min, op1=ALU.mult,
                )
                if last:
                    nc.sync.dma_start(out=out[b, c, :, cols], in_=res[:, cols])
            if not last:
                nc.sync.dma_start(out=out[b, c], in_=res[:])

        def density_round(c):
            for hh in range(HH):
                density(1, c, hh)
                if c + 2 < C:
                    group("m", 1, c + 2, hh)

        def data_round(b, c):
            normalise(b, c)
            nb, nxt = (b, c + 2) if c + 2 < C else (b + 1, c + 2 - C)
            if nb < B:
                for hh in range(HH):
                    group("a", nb, nxt, hh)

        def ky_step(r):
            if r + 1 < B * HH * KP:
                ky_squares(r + 1)
            ky_exp(r)
            ky_quantise(r)

        kx_squares(0)
        kx_squares(1)
        kx_exp(0)
        ky_squares(0)
        kx_exp(1)
        weights(0)
        kx_round(0)
        left("m", 0, 0)
        weights(1)
        left_quantise("m", 0, 0)
        left("m", 0, 1)
        left_quantise("m", 0, 1)
        ky_step(0)
        left("a", 0, 0)
        ky_step(1)
        for c in range(4):
            group("m", 0, c, 0)
        left("a", 0, 1)
        ky_step(2)
        for c in range(4):
            density(0, c, 0)
            group("m", 0, c + 4, 0)
        left_quantise("a", 0, 0)
        ky_step(3)
        left_quantise("a", 0, 1)
        for c in range(4):
            density(0, c + 4, 0)
            group("m", 0, c, 1)
        ky_step(4)
        for c in range(4):
            density(0, c, 1)
            group("m", 0, c + 4, 1)
        for c in range(4, 6):
            density(0, c, 1)
        ky_step(5)
        for c in range(6, 8):
            density(0, c, 1)
        for c in range(2):
            for hh in range(HH):
                group("a", 0, c, hh)
        kx_round(1)
        left("m", 1, 0)
        ky_step(6)
        left_quantise("m", 1, 0)
        left("m", 1, 1)
        ky_step(7)
        nc.vector.tensor_scalar(
            out=tiny[:], in0=ky_tiles[B * HH * KP - 1][:, 0, 0:1], scalar1=0.0, scalar2=TINY, op0=ALU.mult, op1=ALU.add
        )
        left_quantise("m", 1, 1)
        for c in range(2):
            for hh in range(HH):
                group("m", 1, c, hh)
        left("a", 1, 0)
        left("a", 1, 1)
        reciprocals(0)
        for c in range(4):
            density_round(c)
        for c in range(4):
            data_round(0, c)
        for c in range(4, 8):
            density_round(c)
        for c in range(4, 6):
            data_round(0, c)
        left_quantise("a", 1, 0)
        left_quantise("a", 1, 1)
        for c in range(6, 8):
            data_round(0, c)
        reciprocals(1)
        for c in range(C):
            data_round(1, c)
